import numpy as np
import ml_dtypes


def mxq(x, axis, fmt="e4m3"):
    dtype, down = {"e4m3": (ml_dtypes.float8_e4m3fn, 7), "e5m2": (ml_dtypes.float8_e5m2, 14)}[fmt]
    v = np.moveaxis(np.asarray(x, np.float32).astype(ml_dtypes.bfloat16).astype(np.float64), axis, -1)
    blocks = v.reshape(v.shape[:-1] + (-1, 32))
    amax = np.abs(blocks).max(-1, keepdims=True)
    byte = np.maximum(np.where(amax > 0, np.frexp(amax)[1] - 1 + 127, 0) - down, 1)
    scale = np.exp2(byte - 127.0)
    codes = (blocks / scale).astype(np.float32).astype(dtype).astype(np.float64)
    return np.moveaxis((codes * scale).reshape(v.shape), -1, axis)


WIDE = False


def mx_kscale(k):
    if not WIDE:
        return np.ones(k)
    levels = np.array([10, -10, 5, -5, 0])
    a = np.random.permutation(np.resize(levels, k // 512 * 4)).reshape(k // 512, 4)
    idx = np.arange(k)
    return np.exp2(a[idx // 512, idx % 128 // 32])


BF16 = ml_dtypes.bfloat16


def bf(x):
    return np.asarray(x, np.float32).astype(BF16)


def f64(x):
    return np.asarray(x).astype(np.float64)


E2M1 = np.array([0.0, 0.5, 1.0, 1.5, 2.0, 3.0, 4.0, 6.0, -0.0, -0.5, -1.0, -1.5, -2.0, -3.0, -4.0, -6.0])


def pack_weight(w, fmt):
    k, n = w.shape
    w = f64(bf(w)).reshape(k // 32, 32, n)
    amax = np.abs(w).max(1)
    if fmt == "e4m3":
        byte = np.frexp(amax)[1] - 1 + 127 - 7
    else:
        mant, ex = np.frexp(amax / 6.0)
        byte = np.where(mant > 0.5, ex, ex - 1) + 127
    byte = np.clip(np.where(amax > 0, byte, 1), 1, 254)
    scaled = (w * np.exp2(127.0 - byte)[:, None, :]).reshape(k, n).astype(np.float32)
    by_word = np.ascontiguousarray(scaled.reshape(k // 512, 128, 4, n).transpose(0, 1, 3, 2))
    if fmt == "e4m3":
        words = by_word.astype(ml_dtypes.float8_e4m3fn).view(np.uint8)
    else:
        c = by_word.astype(ml_dtypes.float4_e2m1fn).view(np.uint8) & 0xF
        words = c[..., 0::2] | (c[..., 1::2] << 4)
    return np.ascontiguousarray(words), np.ascontiguousarray(byte.astype(np.uint8).reshape(k // 512, 16, n))


def unpack_weight(words, scales, fmt):
    g, p, n, _ = words.shape
    if fmt == "e4m3":
        vals = np.ascontiguousarray(words).view(ml_dtypes.float8_e4m3fn).astype(np.float64)
    else:
        nib = np.empty((g, p, n, 4), np.uint8)
        nib[..., 0::2] = words & 0xF
        nib[..., 1::2] = words >> 4
        vals = E2M1[nib]
    vals = vals * np.repeat(np.exp2(scales.astype(np.float64) - 127.0), 8, axis=1)[..., None]
    return vals.transpose(0, 1, 3, 2).reshape(g * 512, n)


B, D, E, H, L = 512, 512, 16, 512, 128
NOISE_EPS = 0.01
MEAN_EPS = 1e-8
FMT = "e4m3"


def softplus(z):
    return np.log(1.0 + np.exp(z))


def noisy_gates(clean_logits, noise_pre, noise):
    sd = softplus(noise_pre) + NOISE_EPS
    l = clean_logits + noise * sd
    e = np.exp(l - l.max(1, keepdims=True))
    p = e / e.sum(1, keepdims=True)
    m = p.mean(-1) - MEAN_EPS
    g = np.where(p >= m[:, None], p, 0.0)
    return g / g.sum(-1, keepdims=True)


def setup_inputs():
    s = mx_kscale(D)
    x = bf(np.random.standard_normal((B, D)) * s)
    noise = bf(np.random.standard_normal((B, E)))
    clean_logits = bf(np.random.standard_normal((B, E)))
    noise_pre = bf(np.random.standard_normal((B, E)))
    W1 = np.random.standard_normal((E, D, H)) / np.sqrt(D) / s[None, :, None]
    b1 = bf(np.random.standard_normal((E, H)) * 0.2)
    W2 = np.random.standard_normal((E, H, L)) * 2.0 / np.sqrt(H)
    b2 = bf(np.random.standard_normal((E, L)) * 0.3)
    W1_words, W1_scales = pack_weight(W1.reshape(-1, H), FMT)
    W2_words, W2_scales = pack_weight(W2.reshape(-1, L), FMT)
    return {"x": x,
            "noise": noise,
            "clean_logits": clean_logits,
            "noise_pre": noise_pre,
            "W1_words": W1_words,
            "W1_scales": W1_scales,
            "b1": b1,
            "W2_words": W2_words,
            "W2_scales": W2_scales,
            "b2": b2}


def reference(x, noise, clean_logits, noise_pre, W1_words, W1_scales, b1, W2_words, W2_scales, b2):
    gates = noisy_gates(f64(clean_logits), f64(noise_pre), f64(noise))
    h = np.tanh((mxq(f64(x), 1, "e4m3") @ unpack_weight(W1_words, W1_scales, FMT).reshape(E, D, H)) + f64(b1)[:, None, :])
    y = (mxq(h, 2, "e4m3") @ unpack_weight(W2_words, W2_scales, FMT).reshape(E, H, L)) + f64(b2)[:, None, :]
    return gates[:, :, None] * y.transpose(1, 0, 2)

@@ -1,0 +1,261 @@
+from contextlib import ExitStack
+
+import concourse.mybir as mybir
+from concourse.masks import make_identity
+
+F32 = mybir.dt.float32
+BF16 = mybir.dt.bfloat16
+I32 = mybir.dt.int32
+U32 = mybir.dt.uint32
+U8 = mybir.dt.uint8
+FP8X4 = mybir.dt.float8_e4m3fn_x4
+ALU = mybir.AluOpType
+ACT = mybir.ActivationFunctionType
+AX = mybir.AxisListType
+
+P = 128
+PACK = 4
+B, D, E, H, L = 512, 512, 16, 512, 128
+ROW_TILES = B // P
+NOISE_EPS = 0.01
+MEAN_EPS = 1e-8
+GROUP = 4
+STORE = 2
+
+FLOPS = 2 * E * B * D * H + 2 * E * B * H * L
+
+
+def tile_mblfe_pa_e_kernel(
+    tc, x, noise, clean_logits, noise_pre, W1_words, W1_scales, b1, W2_words, W2_scales, b2, out
+):
+    nc = tc.nc
+    with ExitStack() as ctx:
+        keep = ctx.enter_context(tc.tile_pool(name="keep", bufs=1))
+        sums = ctx.enter_context(tc.tile_pool(name="sums", bufs=2 * ROW_TILES))
+        acts = ctx.enter_context(tc.tile_pool(name="acts", bufs=3))
+        z_banks = ctx.enter_context(tc.psum_pool(name="z_banks", bufs=4))
+        t_banks = ctx.enter_context(tc.psum_pool(name="t_banks", bufs=3))
+        y_banks = ctx.enter_context(tc.psum_pool(name="y_banks", bufs=1))
+
+        x_sb = keep.tile([P, ROW_TILES, D], BF16)
+        x_grouped = keep.tile([P, ROW_TILES * P * PACK], BF16, align_bytes=64)
+        x_codes = keep.tile([P, B], U32, align_bytes=64)
+        x_plane = keep.tile([P, B], U8, align_bytes=64)
+        w1_codes = keep.tile([P, E, H], U32, align_bytes=64)
+        w1_planes = keep.tile([P, E, H], U8, align_bytes=64)
+        w2_codes = keep.tile([P, E, L], U32, align_bytes=64)
+        w2_planes = keep.tile([P, E, L], U8, align_bytes=64)
+        b1_rows = keep.tile([P, E, H], BF16)
+        b2_rows = keep.tile([P, E, L], BF16)
+        gate_in = keep.tile([P, 3, ROW_TILES, E], BF16)
+        result = keep.tile([P, ROW_TILES, E, L], F32)
+        ident = keep.tile([P, P], F32)
+
+        nc.vector.memset(w1_planes[:].bitcast(I32), 0)
+        nc.vector.memset(w2_planes[:].bitcast(I32), 0)
+        make_identity(nc, ident[:])
+
+        def load_w1(e):
+            nc.sync.dma_start(
+                out=w1_codes[:, e, :].bitcast(I32),
+                in_=W1_words[e].rearrange("p n t -> p (n t)").bitcast(I32),
+            )
+
+        def load_scale_rows(planes, scales):
+            for q in range(4):
+                nc.sync.dma_start(
+                    out=planes[32 * q : 32 * q + 4, :, :].bitcast(I32),
+                    in_=scales[:, 4 * q : 4 * q + 4, :].rearrange("g r n -> r g n").bitcast(I32),
+                )
+
+        nc.sync.dma_start(out=x_sb[:], in_=x.rearrange("(p i) k -> p i k", i=ROW_TILES))
+        load_w1(0)
+        load_scale_rows(w1_planes, W1_scales)
+        load_w1(1)
+        load_scale_rows(w2_planes, W2_scales)
+        nc.sync.dma_start(
+            out=w2_codes[:].bitcast(I32),
+            in_=W2_words.rearrange("g p n t -> p g (n t)").bitcast(I32),
+        )
+        for e in range(2, E):
+            load_w1(e)
+
+        for j, src in enumerate((noise_pre, noise, clean_logits)):
+            nc.scalar.dma_start(out=gate_in[:, j], in_=src.rearrange("(p i) e -> p i e", i=ROW_TILES))
+        b1_flat = b1.rearrange("e n -> (e n)")
+
+        def load_b1(g):
+            nc.scalar.dma_start(
+                out=b1_rows[:, g * GROUP : (g + 1) * GROUP, :].rearrange("p e n -> p (e n)"),
+                in_=b1_flat[g * GROUP * H : (g + 1) * GROUP * H].partition_broadcast(P),
+            )
+
+        load_b1(0)
+        nc.scalar.dma_start(
+            out=b2_rows[:].rearrange("p e l -> p (e l)"),
+            in_=b2.rearrange("e l -> (e l)").partition_broadcast(P),
+        )
+        for g in range(1, E // GROUP):
+            load_b1(g)
+
+        x_words = x_grouped[:].bitcast(F32).rearrange("q (i b u) -> q i b u", i=ROW_TILES, u=2)
+        for half in range(ROW_TILES // 2):
+            xt = t_banks.tile([P, 512], F32, tag="flipped")
+            for i2 in range(2):
+                for u in range(2):
+                    col = (2 * i2 + u) * P
+                    nc.tensor.transpose(
+                        xt[:, col : col + P],
+                        x_sb[:, 2 * half + i2, :].bitcast(F32)[:, u : D // 2 : 2],
+                        ident[:],
+                    )
+            nc.vector.tensor_copy(
+                out=x_words[:, 2 * half : 2 * half + 2],
+                in_=xt[:].rearrange("q (i u b) -> q i b u", i=2, u=2),
+            )
+        nc.vector.quantize_mx(out=x_codes[:].bitcast(FP8X4), scales=x_plane[:], in_=x_grouped[:])
+
+        shape = [P, ROW_TILES, E]
+        pre, noi, cln = gate_in[:, 0], gate_in[:, 1], gate_in[:, 2]
+        mag = keep.tile(shape, F32)
+        nc.scalar.activation(out=mag[:], in_=pre, func=ACT.Abs)
+        decay = keep.tile(shape, F32)
+        nc.scalar.activation(out=decay[:], in_=mag[:], func=ACT.Exp, scale=-1.0)
+        log1p = keep.tile(shape, F32)
+        nc.scalar.activation(out=log1p[:], in_=decay[:], func=ACT.Ln, bias=1.0)
+        softplus = keep.tile(shape, F32)
+        nc.vector.scalar_tensor_tensor(
+            out=softplus[:], in0=pre, scalar=0.0, in1=log1p[:], op0=ALU.max, op1=ALU.add
+        )
+        noisy = keep.tile(shape, F32)
+        nc.vector.scalar_tensor_tensor(
+            out=noisy[:], in0=softplus[:], scalar=NOISE_EPS, in1=noi, op0=ALU.add, op1=ALU.mult
+        )
+        logits = keep.tile(shape, F32)
+        nc.vector.tensor_tensor(out=logits[:], in0=noisy[:], in1=cln, op=ALU.add)
+
+        def over_experts(per_row):
+            return per_row[:].unsqueeze(2).to_broadcast(shape)
+
+        top = keep.tile([P, ROW_TILES], F32)
+        nc.vector.tensor_reduce(out=top[:], in_=logits[:], axis=AX.X, op=ALU.max)
+        shifted = keep.tile(shape, F32)
+        nc.vector.tensor_tensor(out=shifted[:], in0=logits[:], in1=over_experts(top), op=ALU.subtract)
+        expd = keep.tile(shape, F32)
+        nc.scalar.activation(out=expd[:], in_=shifted[:], func=ACT.Exp)
+        esum = keep.tile([P, ROW_TILES], F32)
+        nc.vector.tensor_reduce(out=esum[:], in_=expd[:], axis=AX.X, op=ALU.add)
+        einv = keep.tile([P, ROW_TILES], F32)
+        nc.vector.reciprocal(out=einv[:], in_=esum[:])
+        prob = keep.tile(shape, F32)
+        nc.vector.tensor_tensor(out=prob[:], in0=expd[:], in1=over_experts(einv), op=ALU.mult)
+        psum_row = keep.tile([P, ROW_TILES], F32)
+        nc.vector.tensor_reduce(out=psum_row[:], in_=prob[:], axis=AX.X, op=ALU.add)
+        cut = keep.tile([P, ROW_TILES], F32)
+        nc.vector.tensor_scalar(
+            out=cut[:], in0=psum_row[:], scalar1=1.0 / E, scalar2=-MEAN_EPS, op0=ALU.mult, op1=ALU.add
+        )
+        alive = keep.tile(shape, F32)
+        nc.vector.tensor_tensor(out=alive[:], in0=prob[:], in1=over_experts(cut), op=ALU.is_ge)
+        kept = keep.tile(shape, F32)
+        nc.vector.tensor_tensor(out=kept[:], in0=prob[:], in1=alive[:], op=ALU.mult)
+        ksum = keep.tile([P, ROW_TILES], F32)
+        nc.vector.tensor_reduce(out=ksum[:], in_=kept[:], axis=AX.X, op=ALU.add)
+        kinv = keep.tile([P, ROW_TILES], F32)
+        nc.vector.reciprocal(out=kinv[:], in_=ksum[:])
+        gates = keep.tile(shape, F32)
+        nc.vector.tensor_tensor(out=gates[:], in0=kept[:], in1=over_experts(kinv), op=ALU.mult)
+
+        for g in range(E // GROUP):
+            es = slice(g * GROUP, (g + 1) * GROUP)
+            nc.gpsimd.tensor_tensor(
+                out=result[:, :, es, :],
+                in0=b2_rows[:, es, :].unsqueeze(1).to_broadcast([P, ROW_TILES, GROUP, L]),
+                in1=gates[:, :, es].unsqueeze(3).to_broadcast([P, ROW_TILES, GROUP, L]),
+                op=ALU.mult,
+            )
+
+        out_rows = out.rearrange("(p i) e l -> p i e l", i=ROW_TILES)
+        biased = {}
+        grouped = {}
+        packed = {}
+
+        def first_product(e):
+            for i in range(ROW_TILES):
+                rows = slice(i * P, (i + 1) * P)
+                z = z_banks.tile([P, H], F32)
+                nc.tensor.matmul_mx(
+                    out=z[:],
+                    lhsT=x_codes[:, rows].bitcast(FP8X4),
+                    lhsT_scale=x_plane[:, rows],
+                    rhs=w1_codes[:, e, :].bitcast(FP8X4),
+                    rhs_scale=w1_planes[:, e, :],
+                    start=True,
+                    stop=True,
+                )
+                zb = sums.tile([P, PACK, P], F32)
+                nc.vector.tensor_tensor(
+                    out=zb[:],
+                    in0=z[:].rearrange("b (q t) -> b t q", t=PACK),
+                    in1=b1_rows[:, e, :].rearrange("b (q t) -> b t q", t=PACK),
+                    op=ALU.add,
+                )
+                biased[(e, i)] = zb
+
+        def flip_and_tanh(e):
+            hg = acts.tile([P, ROW_TILES, P, PACK], BF16, align_bytes=64)
+            for i in range(ROW_TILES):
+                zt = t_banks.tile([P, 512], F32, tag="flipped")
+                for t in range(PACK):
+                    nc.tensor.transpose(zt[:, t * P : (t + 1) * P], biased[(e, i)][:, t, :], ident[:])
+                nc.scalar.activation(
+                    out=hg[:, i], in_=zt[:].rearrange("q (t b) -> q b t", t=PACK), func=ACT.Tanh
+                )
+            grouped[e] = hg
+
+        def quantise_hidden(e):
+            h_codes = acts.tile([P, B], U32, align_bytes=64)
+            h_plane = acts.tile([P, B], U8, align_bytes=64)
+            nc.vector.quantize_mx(
+                out=h_codes[:].bitcast(FP8X4),
+                scales=h_plane[:],
+                in_=grouped[e][:].rearrange("q i b t -> q (i b t)"),
+            )
+            packed[e] = (h_codes, h_plane)
+
+        def second_product(e):
+            h_codes, h_plane = packed[e]
+            y = y_banks.tile([P, ROW_TILES, L], F32)
+            for i in range(ROW_TILES):
+                rows = slice(i * P, (i + 1) * P)
+                nc.tensor.matmul_mx(
+                    out=y[:, i, :],
+                    lhsT=h_codes[:, rows].bitcast(FP8X4),
+                    lhsT_scale=h_plane[:, rows],
+                    rhs=w2_codes[:, e, :].bitcast(FP8X4),
+                    rhs_scale=w2_planes[:, e, :],
+                    start=True,
+                    stop=True,
+                )
+            for i in range(ROW_TILES):
+                nc.vector.scalar_tensor_tensor(
+                    out=result[:, i, e, :],
+                    in0=y[:, i, :],
+                    scalar=gates[:, i, e : e + 1],
+                    in1=result[:, i, e, :],
+                    op0=ALU.mult,
+                    op1=ALU.add,
+                )
+            if e % STORE == STORE - 1:
+                es = slice(e + 1 - STORE, e + 1)
+                nc.sync.dma_start(out=out_rows[:, :, es, :], in_=result[:, :, es, :])
+
+        for step in range(E + 2):
+            if step >= 2:
+                quantise_hidden(step - 2)
+            if step < E:
+                first_product(step)
+            if 1 <= step <= E:
+                flip_and_tanh(step - 1)
+            if step >= 2:
+                second_product(step - 2)

@@ -36,6 +36,7 @@ def tile_mblfe_pa_e_kernel(
         z_banks = ctx.enter_context(tc.psum_pool(name="z_banks", bufs=4))
         t_banks = ctx.enter_context(tc.psum_pool(name="t_banks", bufs=3))
         y_banks = ctx.enter_context(tc.psum_pool(name="y_banks", bufs=1))
+        ctx.enter_context(tc.manual_schedule())
 
         x_sb = keep.tile([P, ROW_TILES, D], BF16)
         x_grouped = keep.tile([P, ROW_TILES * P * PACK], BF16, align_bytes=64)
@@ -143,42 +144,36 @@ def tile_mblfe_pa_e_kernel(
         nc.vector.tensor_tensor(out=shifted[:], in0=logits[:], in1=over_experts(top), op=ALU.subtract)
         expd = keep.tile(shape, F32)
         nc.scalar.activation(out=expd[:], in_=shifted[:], func=ACT.Exp)
-        esum = keep.tile([P, ROW_TILES], F32)
-        nc.vector.tensor_reduce(out=esum[:], in_=expd[:], axis=AX.X, op=ALU.add)
-        einv = keep.tile([P, ROW_TILES], F32)
-        nc.vector.reciprocal(out=einv[:], in_=esum[:])
-        prob = keep.tile(shape, F32)
-        nc.vector.tensor_tensor(out=prob[:], in0=expd[:], in1=over_experts(einv), op=ALU.mult)
-        psum_row = keep.tile([P, ROW_TILES], F32)
-        nc.vector.tensor_reduce(out=psum_row[:], in_=prob[:], axis=AX.X, op=ALU.add)
-        cut = keep.tile([P, ROW_TILES], F32)
-        nc.vector.tensor_scalar(
-            out=cut[:], in0=psum_row[:], scalar1=1.0 / E, scalar2=-MEAN_EPS, op0=ALU.mult, op1=ALU.add
-        )
-        alive = keep.tile(shape, F32)
-        nc.vector.tensor_tensor(out=alive[:], in0=prob[:], in1=over_experts(cut), op=ALU.is_ge)
-        kept = keep.tile(shape, F32)
-        nc.vector.tensor_tensor(out=kept[:], in0=prob[:], in1=alive[:], op=ALU.mult)
-        ksum = keep.tile([P, ROW_TILES], F32)
-        nc.vector.tensor_reduce(out=ksum[:], in_=kept[:], axis=AX.X, op=ALU.add)
-        kinv = keep.tile([P, ROW_TILES], F32)
-        nc.vector.reciprocal(out=kinv[:], in_=ksum[:])
         gates = keep.tile(shape, F32)
-        nc.vector.tensor_tensor(out=gates[:], in0=kept[:], in1=over_experts(kinv), op=ALU.mult)
 
-        for g in range(E // GROUP):
-            es = slice(g * GROUP, (g + 1) * GROUP)
-            nc.gpsimd.tensor_tensor(
-                out=result[:, :, es, :],
-                in0=b2_rows[:, es, :].unsqueeze(1).to_broadcast([P, ROW_TILES, GROUP, L]),
-                in1=gates[:, :, es].unsqueeze(3).to_broadcast([P, ROW_TILES, GROUP, L]),
-                op=ALU.mult,
+        def finish_gates():
+            esum = keep.tile([P, ROW_TILES], F32)
+            nc.vector.tensor_reduce(out=esum[:], in_=expd[:], axis=AX.X, op=ALU.add)
+            einv = keep.tile([P, ROW_TILES], F32)
+            nc.vector.reciprocal(out=einv[:], in_=esum[:])
+            prob = keep.tile(shape, F32)
+            nc.vector.tensor_tensor(out=prob[:], in0=expd[:], in1=over_experts(einv), op=ALU.mult)
+            psum_row = keep.tile([P, ROW_TILES], F32)
+            nc.vector.tensor_reduce(out=psum_row[:], in_=prob[:], axis=AX.X, op=ALU.add)
+            cut = keep.tile([P, ROW_TILES], F32)
+            nc.vector.tensor_scalar(
+                out=cut[:], in0=psum_row[:], scalar1=1.0 / E, scalar2=-MEAN_EPS, op0=ALU.mult, op1=ALU.add
             )
+            alive = keep.tile(shape, F32)
+            nc.vector.tensor_tensor(out=alive[:], in0=prob[:], in1=over_experts(cut), op=ALU.is_ge)
+            kept = keep.tile(shape, F32)
+            nc.vector.tensor_tensor(out=kept[:], in0=prob[:], in1=alive[:], op=ALU.mult)
+            ksum = keep.tile([P, ROW_TILES], F32)
+            nc.vector.tensor_reduce(out=ksum[:], in_=kept[:], axis=AX.X, op=ALU.add)
+            kinv = keep.tile([P, ROW_TILES], F32)
+            nc.vector.reciprocal(out=kinv[:], in_=ksum[:])
+            nc.vector.tensor_tensor(out=gates[:], in0=kept[:], in1=over_experts(kinv), op=ALU.mult)
 
         out_rows = out.rearrange("(p i) e l -> p i e l", i=ROW_TILES)
         biased = {}
         grouped = {}
         packed = {}
+        products = {}
 
         def first_product(e):
             for i in range(ROW_TILES):
@@ -237,25 +232,34 @@ def tile_mblfe_pa_e_kernel(
                     start=True,
                     stop=True,
                 )
+            products[e] = y
+
+        def weigh_and_store(e):
+            yb = acts.tile([P, ROW_TILES, L], F32)
+            nc.vector.tensor_tensor(
+                out=yb[:],
+                in0=products[e][:],
+                in1=b2_rows[:, e, :].unsqueeze(1).to_broadcast([P, ROW_TILES, L]),
+                op=ALU.add,
+            )
             for i in range(ROW_TILES):
-                nc.vector.scalar_tensor_tensor(
-                    out=result[:, i, e, :],
-                    in0=y[:, i, :],
-                    scalar=gates[:, i, e : e + 1],
-                    in1=result[:, i, e, :],
-                    op0=ALU.mult,
-                    op1=ALU.add,
+                nc.scalar.activation(
+                    out=result[:, i, e, :], in_=yb[:, i, :], func=ACT.Copy, scale=gates[:, i, e : e + 1]
                 )
             if e % STORE == STORE - 1:
                 es = slice(e + 1 - STORE, e + 1)
                 nc.sync.dma_start(out=out_rows[:, :, es, :], in_=result[:, :, es, :])
 
-        for step in range(E + 2):
-            if step >= 2:
+        for step in range(E + 3):
+            if 0 <= step - 2 < E:
                 quantise_hidden(step - 2)
+            if 0 <= step - 1 < E:
+                flip_and_tanh(step - 1)
+            if 0 <= step - 3 < E:
+                weigh_and_store(step - 3)
             if step < E:
                 first_product(step)
-            if 1 <= step <= E:
-                flip_and_tanh(step - 1)
-            if step >= 2:
+            if step == 0:
+                finish_gates()
+            if 0 <= step - 2 < E:
                 second_product(step - 2)

@@ -19,7 +19,7 @@ B, D, E, H, L = 512, 512, 16, 512, 128
 ROW_TILES = B // P
 NOISE_EPS = 0.01
 MEAN_EPS = 1e-8
-GROUP = 4
+B2_ROW = E
 STORE = 2
 
 FLOPS = 2 * E * B * D * H + 2 * E * B * H * L
@@ -33,9 +33,10 @@ def tile_mblfe_pa_e_kernel(
         keep = ctx.enter_context(tc.tile_pool(name="keep", bufs=1))
         sums = ctx.enter_context(tc.tile_pool(name="sums", bufs=2 * ROW_TILES))
         acts = ctx.enter_context(tc.tile_pool(name="acts", bufs=3))
-        z_banks = ctx.enter_context(tc.psum_pool(name="z_banks", bufs=4))
+        z_banks = ctx.enter_context(tc.psum_pool(name="z_banks", bufs=3))
         t_banks = ctx.enter_context(tc.psum_pool(name="t_banks", bufs=3))
         y_banks = ctx.enter_context(tc.psum_pool(name="y_banks", bufs=1))
+        bias_banks = ctx.enter_context(tc.psum_pool(name="bias_banks", bufs=1))
         ctx.enter_context(tc.manual_schedule())
 
         x_sb = keep.tile([P, ROW_TILES, D], BF16)
@@ -51,9 +52,13 @@ def tile_mblfe_pa_e_kernel(
         gate_in = keep.tile([P, 3, ROW_TILES, E], BF16)
         result = keep.tile([P, ROW_TILES, E, L], F32)
         ident = keep.tile([P, P], F32)
+        ident_bf = keep.tile([P, P], BF16)
+        bias_in = keep.tile([P, H], BF16)
 
         nc.vector.memset(w1_planes[:].bitcast(I32), 0)
         nc.vector.memset(w2_planes[:].bitcast(I32), 0)
+        nc.gpsimd.memset(bias_in[:], 0.0)
+        make_identity(nc, ident_bf[:])
         make_identity(nc, ident[:])
 
         def load_w1(e):
@@ -81,23 +86,34 @@ def tile_mblfe_pa_e_kernel(
         for e in range(2, E):
             load_w1(e)
 
+        nc.scalar.dma_start(out=bias_in[0:E, :], in_=b1)
+        nc.scalar.dma_start(
+            out=bias_in[B2_ROW : B2_ROW + 4, :], in_=b2.rearrange("(g e) l -> g (e l)", g=4)
+        )
         for j, src in enumerate((noise_pre, noise, clean_logits)):
             nc.scalar.dma_start(out=gate_in[:, j], in_=src.rearrange("(p i) e -> p i e", i=ROW_TILES))
-        b1_flat = b1.rearrange("e n -> (e n)")
 
-        def load_b1(g):
-            nc.scalar.dma_start(
-                out=b1_rows[:, g * GROUP : (g + 1) * GROUP, :].rearrange("p e n -> p (e n)"),
-                in_=b1_flat[g * GROUP * H : (g + 1) * GROUP * H].partition_broadcast(P),
+        def spread_two_rows(row, dest):
+            bank = bias_banks.tile([P, 2, H], BF16)
+            for j in range(2):
+                nc.tensor.matmul(
+                    out=bank[:, j, :],
+                    lhsT=ident_bf[:, row + j : row + j + 1].to_broadcast([P, P]),
+                    rhs=bias_in[:],
+                    start=True,
+                    stop=True,
+                )
+            nc.scalar.copy(out=dest, in_=bank[:].rearrange("p j n -> p (j n)"))
+
+        def spread_b1(e):
+            spread_two_rows(e, b1_rows[:, e : e + 2, :].rearrange("p e n -> p (e n)"))
+
+        def spread_b2(half):
+            spread_two_rows(
+                B2_ROW + 2 * half, b2_rows[:, 8 * half : 8 * half + 8, :].rearrange("p e l -> p (e l)")
             )
 
-        load_b1(0)
-        nc.scalar.dma_start(
-            out=b2_rows[:].rearrange("p e l -> p (e l)"),
-            in_=b2.rearrange("e l -> (e l)").partition_broadcast(P),
-        )
-        for g in range(1, E // GROUP):
-            load_b1(g)
+        spread_b1(0)
 
         x_words = x_grouped[:].bitcast(F32).rearrange("q (i b u) -> q i b u", i=ROW_TILES, u=2)
         for half in range(ROW_TILES // 2):
@@ -255,6 +271,10 @@ def tile_mblfe_pa_e_kernel(
                 quantise_hidden(step - 2)
             if 0 <= step - 1 < E:
                 flip_and_tanh(step - 1)
+            if step % 2 == 0 and step + 2 < E:
+                spread_b1(step + 2)
+            if step % 2 == 1 and step < 4:
+                spread_b2(step // 2)
             if 0 <= step - 3 < E:
                 weigh_and_store(step - 3)
             if step < E:

@@ -19,7 +19,7 @@ B, D, E, H, L = 512, 512, 16, 512, 128
 ROW_TILES = B // P
 NOISE_EPS = 0.01
 MEAN_EPS = 1e-8
-B2_ROW = E
+GROUP = 4
 STORE = 2
 
 FLOPS = 2 * E * B * D * H + 2 * E * B * H * L
@@ -33,10 +33,9 @@ def tile_mblfe_pa_e_kernel(
         keep = ctx.enter_context(tc.tile_pool(name="keep", bufs=1))
         sums = ctx.enter_context(tc.tile_pool(name="sums", bufs=2 * ROW_TILES))
         acts = ctx.enter_context(tc.tile_pool(name="acts", bufs=3))
-        z_banks = ctx.enter_context(tc.psum_pool(name="z_banks", bufs=3))
+        z_banks = ctx.enter_context(tc.psum_pool(name="z_banks", bufs=4))
         t_banks = ctx.enter_context(tc.psum_pool(name="t_banks", bufs=3))
         y_banks = ctx.enter_context(tc.psum_pool(name="y_banks", bufs=1))
-        bias_banks = ctx.enter_context(tc.psum_pool(name="bias_banks", bufs=1))
         ctx.enter_context(tc.manual_schedule())
 
         x_sb = keep.tile([P, ROW_TILES, D], BF16)
@@ -52,13 +51,9 @@ def tile_mblfe_pa_e_kernel(
         gate_in = keep.tile([P, 3, ROW_TILES, E], BF16)
         result = keep.tile([P, ROW_TILES, E, L], F32)
         ident = keep.tile([P, P], F32)
-        ident_bf = keep.tile([P, P], BF16)
-        bias_in = keep.tile([P, H], BF16)
 
         nc.vector.memset(w1_planes[:].bitcast(I32), 0)
         nc.vector.memset(w2_planes[:].bitcast(I32), 0)
-        nc.gpsimd.memset(bias_in[:], 0.0)
-        make_identity(nc, ident_bf[:])
         make_identity(nc, ident[:])
 
         def load_w1(e):
@@ -86,34 +81,23 @@ def tile_mblfe_pa_e_kernel(
         for e in range(2, E):
             load_w1(e)
 
-        nc.scalar.dma_start(out=bias_in[0:E, :], in_=b1)
-        nc.scalar.dma_start(
-            out=bias_in[B2_ROW : B2_ROW + 4, :], in_=b2.rearrange("(g e) l -> g (e l)", g=4)
-        )
         for j, src in enumerate((noise_pre, noise, clean_logits)):
             nc.scalar.dma_start(out=gate_in[:, j], in_=src.rearrange("(p i) e -> p i e", i=ROW_TILES))
+        b1_flat = b1.rearrange("e n -> (e n)")
 
-        def spread_two_rows(row, dest):
-            bank = bias_banks.tile([P, 2, H], BF16)
-            for j in range(2):
-                nc.tensor.matmul(
-                    out=bank[:, j, :],
-                    lhsT=ident_bf[:, row + j : row + j + 1].to_broadcast([P, P]),
-                    rhs=bias_in[:],
-                    start=True,
-                    stop=True,
-                )
-            nc.scalar.copy(out=dest, in_=bank[:].rearrange("p j n -> p (j n)"))
-
-        def spread_b1(e):
-            spread_two_rows(e, b1_rows[:, e : e + 2, :].rearrange("p e n -> p (e n)"))
-
-        def spread_b2(half):
-            spread_two_rows(
-                B2_ROW + 2 * half, b2_rows[:, 8 * half : 8 * half + 8, :].rearrange("p e l -> p (e l)")
+        def load_b1(g):
+            nc.scalar.dma_start(
+                out=b1_rows[:, g * GROUP : (g + 1) * GROUP, :].rearrange("p e n -> p (e n)"),
+                in_=b1_flat[g * GROUP * H : (g + 1) * GROUP * H].partition_broadcast(P),
             )
 
-        spread_b1(0)
+        load_b1(0)
+        nc.scalar.dma_start(
+            out=b2_rows[:].rearrange("p e l -> p (e l)"),
+            in_=b2.rearrange("e l -> (e l)").partition_broadcast(P),
+        )
+        for g in range(1, E // GROUP):
+            load_b1(g)
 
         x_words = x_grouped[:].bitcast(F32).rearrange("q (i b u) -> q i b u", i=ROW_TILES, u=2)
         for half in range(ROW_TILES // 2):
@@ -206,9 +190,9 @@ def tile_mblfe_pa_e_kernel(
                 )
                 zb = sums.tile([P, PACK, P], F32)
                 nc.vector.tensor_tensor(
-                    out=zb[:],
-                    in0=z[:].rearrange("b (q t) -> b t q", t=PACK),
-                    in1=b1_rows[:, e, :].rearrange("b (q t) -> b t q", t=PACK),
+                    out=zb[:].rearrange("b t q -> b q t"),
+                    in0=z[:].rearrange("b (q t) -> b q t", t=PACK),
+                    in1=b1_rows[:, e, :].rearrange("b (q t) -> b q t", t=PACK),
                     op=ALU.add,
                 )
                 biased[(e, i)] = zb
@@ -271,10 +255,6 @@ def tile_mblfe_pa_e_kernel(
                 quantise_hidden(step - 2)
             if 0 <= step - 1 < E:
                 flip_and_tanh(step - 1)
-            if step % 2 == 0 and step + 2 < E:
-                spread_b1(step + 2)
-            if step % 2 == 1 and step < 4:
-                spread_b2(step // 2)
             if 0 <= step - 3 < E:
                 weigh_and_store(step - 3)
             if step < E:

@@ -69,7 +69,9 @@ def tile_mblfe_pa_e_kernel(
                     in_=scales[:, 4 * q : 4 * q + 4, :].rearrange("g r n -> r g n").bitcast(I32),
                 )
 
-        nc.sync.dma_start(out=x_sb[:], in_=x.rearrange("(p i) k -> p i k", i=ROW_TILES))
+        x_rows = x.rearrange("(p i) k -> p i k", i=ROW_TILES)
+        for i in range(ROW_TILES):
+            nc.sync.dma_start(out=x_sb[:, i, :], in_=x_rows[:, i, :])
         load_w1(0)
         load_scale_rows(w1_planes, W1_scales)
         load_w1(1)
@@ -100,21 +102,17 @@ def tile_mblfe_pa_e_kernel(
             load_b1(g)
 
         x_words = x_grouped[:].bitcast(F32).rearrange("q (i b u) -> q i b u", i=ROW_TILES, u=2)
-        for half in range(ROW_TILES // 2):
-            xt = t_banks.tile([P, 512], F32, tag="flipped")
-            for i2 in range(2):
-                for u in range(2):
-                    col = (2 * i2 + u) * P
-                    nc.tensor.transpose(
-                        xt[:, col : col + P],
-                        x_sb[:, 2 * half + i2, :].bitcast(F32)[:, u : D // 2 : 2],
-                        ident[:],
-                    )
-            nc.vector.tensor_copy(
-                out=x_words[:, 2 * half : 2 * half + 2],
-                in_=xt[:].rearrange("q (i u b) -> q i b u", i=2, u=2),
+        for i in range(ROW_TILES):
+            rows = slice(i * P, (i + 1) * P)
+            xt = t_banks.tile([P, 2, P], F32, tag="flipped")
+            for u in range(2):
+                nc.tensor.transpose(xt[:, u, :], x_sb[:, i, :].bitcast(F32)[:, u : D // 2 : 2], ident[:])
+            nc.vector.tensor_copy(out=x_words[:, i], in_=xt[:].rearrange("q u b -> q b u"))
+            nc.vector.quantize_mx(
+                out=x_codes[:, rows].bitcast(FP8X4),
+                scales=x_plane[:, rows],
+                in_=x_grouped[:, i * P * PACK : (i + 1) * P * PACK],
             )
-        nc.vector.quantize_mx(out=x_codes[:].bitcast(FP8X4), scales=x_plane[:], in_=x_grouped[:])
 
         shape = [P, ROW_TILES, E]
         pre, noi, cln = gate_in[:, 0], gate_in[:, 1], gate_in[:, 2]
@@ -190,9 +188,9 @@ def tile_mblfe_pa_e_kernel(
                 )
                 zb = sums.tile([P, PACK, P], F32)
                 nc.vector.tensor_tensor(
-                    out=zb[:].rearrange("b t q -> b q t"),
-                    in0=z[:].rearrange("b (q t) -> b q t", t=PACK),
-                    in1=b1_rows[:, e, :].rearrange("b (q t) -> b q t", t=PACK),
+                    out=zb[:],
+                    in0=z[:].rearrange("b (q t) -> b t q", t=PACK),
+                    in1=b1_rows[:, e, :].rearrange("b (q t) -> b t q", t=PACK),
                     op=ALU.add,
                 )
                 biased[(e, i)] = zb
@@ -232,34 +230,37 @@ def tile_mblfe_pa_e_kernel(
                     start=True,
                     stop=True,
                 )
-            products[e] = y
-
-        def weigh_and_store(e):
             yb = acts.tile([P, ROW_TILES, L], F32)
             nc.vector.tensor_tensor(
                 out=yb[:],
-                in0=products[e][:],
+                in0=y[:],
                 in1=b2_rows[:, e, :].unsqueeze(1).to_broadcast([P, ROW_TILES, L]),
                 op=ALU.add,
             )
+            products[e] = yb
+
+        def weigh_and_store(e):
             for i in range(ROW_TILES):
                 nc.scalar.activation(
-                    out=result[:, i, e, :], in_=yb[:, i, :], func=ACT.Copy, scale=gates[:, i, e : e + 1]
+                    out=result[:, i, e, :],
+                    in_=products[e][:, i, :],
+                    func=ACT.Copy,
+                    scale=gates[:, i, e : e + 1],
                 )
             if e % STORE == STORE - 1:
                 es = slice(e + 1 - STORE, e + 1)
                 nc.sync.dma_start(out=out_rows[:, :, es, :], in_=result[:, :, es, :])
 
-        for step in range(E + 3):
-            if 0 <= step - 2 < E:
-                quantise_hidden(step - 2)
-            if 0 <= step - 1 < E:
-                flip_and_tanh(step - 1)
-            if 0 <= step - 3 < E:
-                weigh_and_store(step - 3)
+        for step in range(E + 4):
             if step < E:
                 first_product(step)
             if step == 0:
                 finish_gates()
+            if 0 <= step - 1 < E:
+                flip_and_tanh(step - 1)
+            if 0 <= step - 4 < E:
+                weigh_and_store(step - 4)
             if 0 <= step - 2 < E:
-                second_product(step - 2)
+                quantise_hidden(step - 2)
+            if 0 <= step - 3 < E:
+                second_product(step - 3)

@@ -230,23 +230,24 @@ def tile_mblfe_pa_e_kernel(
                     start=True,
                     stop=True,
                 )
-            yb = acts.tile([P, ROW_TILES, L], F32)
-            nc.vector.tensor_tensor(
-                out=yb[:],
-                in0=y[:],
+            y_sb = acts.tile([P, ROW_TILES, L], F32)
+            nc.scalar.copy(out=y_sb[:], in_=y[:])
+            products[e] = y_sb
+
+        def weigh_and_store(e):
+            y_sb = products[e]
+            nc.gpsimd.tensor_tensor(
+                out=y_sb[:],
+                in0=y_sb[:],
                 in1=b2_rows[:, e, :].unsqueeze(1).to_broadcast([P, ROW_TILES, L]),
                 op=ALU.add,
             )
-            products[e] = yb
-
-        def weigh_and_store(e):
-            for i in range(ROW_TILES):
-                nc.scalar.activation(
-                    out=result[:, i, e, :],
-                    in_=products[e][:, i, :],
-                    func=ACT.Copy,
-                    scale=gates[:, i, e : e + 1],
-                )
+            nc.gpsimd.tensor_tensor(
+                out=result[:, :, e, :],
+                in0=y_sb[:],
+                in1=gates[:, :, e : e + 1].to_broadcast([P, ROW_TILES, L]),
+                op=ALU.mult,
+            )
             if e % STORE == STORE - 1:
                 es = slice(e + 1 - STORE, e + 1)
                 nc.sync.dma_start(out=out_rows[:, :, es, :], in_=result[:, :, es, :])

@@ -21,6 +21,7 @@ NOISE_EPS = 0.01
 MEAN_EPS = 1e-8
 GROUP = 4
 STORE = 2
+RUN = 2
 
 FLOPS = 2 * E * B * D * H + 2 * E * B * H * L
 
@@ -173,8 +174,8 @@ def tile_mblfe_pa_e_kernel(
         packed = {}
         products = {}
 
-        def first_product(e):
-            for i in range(ROW_TILES):
+        def first_product(e, tiles):
+            for i in tiles:
                 rows = slice(i * P, (i + 1) * P)
                 z = z_banks.tile([P, H], F32)
                 nc.tensor.matmul_mx(
@@ -195,16 +196,18 @@ def tile_mblfe_pa_e_kernel(
                 )
                 biased[(e, i)] = zb
 
-        def flip_and_tanh(e):
-            hg = acts.tile([P, ROW_TILES, P, PACK], BF16, align_bytes=64)
-            for i in range(ROW_TILES):
+        def flip_and_tanh(e, tiles):
+            if e not in grouped:
+                hg = acts.tile([P, ROW_TILES, P, PACK], BF16, align_bytes=64)
+                grouped[e] = hg
+            hg = grouped[e]
+            for i in tiles:
                 zt = t_banks.tile([P, 512], F32, tag="flipped")
                 for t in range(PACK):
                     nc.tensor.transpose(zt[:, t * P : (t + 1) * P], biased[(e, i)][:, t, :], ident[:])
                 nc.scalar.activation(
                     out=hg[:, i], in_=zt[:].rearrange("q (t b) -> q b t", t=PACK), func=ACT.Tanh
                 )
-            grouped[e] = hg
 
         def quantise_hidden(e):
             h_codes = acts.tile([P, B], U32, align_bytes=64)
@@ -230,35 +233,36 @@ def tile_mblfe_pa_e_kernel(
                     start=True,
                     stop=True,
                 )
-            y_sb = acts.tile([P, ROW_TILES, L], F32)
-            nc.scalar.copy(out=y_sb[:], in_=y[:])
-            products[e] = y_sb
-
-        def weigh_and_store(e):
-            y_sb = products[e]
-            nc.gpsimd.tensor_tensor(
-                out=y_sb[:],
-                in0=y_sb[:],
+            yb = acts.tile([P, ROW_TILES, L], F32)
+            nc.vector.tensor_tensor(
+                out=yb[:],
+                in0=y[:],
                 in1=b2_rows[:, e, :].unsqueeze(1).to_broadcast([P, ROW_TILES, L]),
                 op=ALU.add,
             )
-            nc.gpsimd.tensor_tensor(
-                out=result[:, :, e, :],
-                in0=y_sb[:],
-                in1=gates[:, :, e : e + 1].to_broadcast([P, ROW_TILES, L]),
-                op=ALU.mult,
-            )
+            products[e] = yb
+
+        def weigh_and_store(e):
+            for i in range(ROW_TILES):
+                nc.scalar.activation(
+                    out=result[:, i, e, :],
+                    in_=products[e][:, i, :],
+                    func=ACT.Copy,
+                    scale=gates[:, i, e : e + 1],
+                )
             if e % STORE == STORE - 1:
                 es = slice(e + 1 - STORE, e + 1)
                 nc.sync.dma_start(out=out_rows[:, :, es, :], in_=result[:, :, es, :])
 
         for step in range(E + 4):
-            if step < E:
-                first_product(step)
+            for first in range(0, ROW_TILES, RUN):
+                tiles = range(first, first + RUN)
+                if step < E:
+                    first_product(step, tiles)
+                if 0 <= step - 1 < E:
+                    flip_and_tanh(step - 1, tiles)
             if step == 0:
                 finish_gates()
-            if 0 <= step - 1 < E:
-                flip_and_tanh(step - 1)
             if 0 <= step - 4 < E:
                 weigh_and_store(step - 4)
             if 0 <= step - 2 < E:

@@ -19,9 +19,8 @@ B, D, E, H, L = 512, 512, 16, 512, 128
 ROW_TILES = B // P
 NOISE_EPS = 0.01
 MEAN_EPS = 1e-8
-GROUP = 4
+PLANES = 4
 STORE = 2
-RUN = 2
 
 FLOPS = 2 * E * B * D * H + 2 * E * B * H * L
 
@@ -32,88 +31,120 @@ def tile_mblfe_pa_e_kernel(
     nc = tc.nc
     with ExitStack() as ctx:
         keep = ctx.enter_context(tc.tile_pool(name="keep", bufs=1))
-        sums = ctx.enter_context(tc.tile_pool(name="sums", bufs=2 * ROW_TILES))
         acts = ctx.enter_context(tc.tile_pool(name="acts", bufs=3))
-        z_banks = ctx.enter_context(tc.psum_pool(name="z_banks", bufs=4))
-        t_banks = ctx.enter_context(tc.psum_pool(name="t_banks", bufs=3))
-        y_banks = ctx.enter_context(tc.psum_pool(name="y_banks", bufs=1))
+        z_banks = ctx.enter_context(tc.psum_pool(name="z_banks", bufs=6))
+        y_banks = ctx.enter_context(tc.psum_pool(name="y_banks", bufs=2))
         ctx.enter_context(tc.manual_schedule())
 
         x_sb = keep.tile([P, ROW_TILES, D], BF16)
         x_grouped = keep.tile([P, ROW_TILES * P * PACK], BF16, align_bytes=64)
         x_codes = keep.tile([P, B], U32, align_bytes=64)
         x_plane = keep.tile([P, B], U8, align_bytes=64)
-        w1_codes = keep.tile([P, E, H], U32, align_bytes=64)
-        w1_planes = keep.tile([P, E, H], U8, align_bytes=64)
+        w1_raw = keep.tile([P, E, H], U32, align_bytes=64)
+        w1_raw_planes = keep.tile([P, E // PLANES, H], U8, align_bytes=64)
+        w1_planes = keep.tile([P, E // PLANES, H], U8, align_bytes=64)
         w2_codes = keep.tile([P, E, L], U32, align_bytes=64)
         w2_planes = keep.tile([P, E, L], U8, align_bytes=64)
-        b1_rows = keep.tile([P, E, H], BF16)
+        b1_rows = keep.tile([P, H], BF16)
+        b1_cols = keep.tile([P, E, PACK], BF16)
         b2_rows = keep.tile([P, E, L], BF16)
         gate_in = keep.tile([P, 3, ROW_TILES, E], BF16)
         result = keep.tile([P, ROW_TILES, E, L], F32)
         ident = keep.tile([P, P], F32)
+        ones = keep.tile([P, 1], F32)
+        warm = keep.tile([P, 1], F32)
 
-        nc.vector.memset(w1_planes[:].bitcast(I32), 0)
+        nc.vector.memset(w1_raw_planes[:].bitcast(I32), 0)
+        nc.vector.memset(ones[:], 1.0)
+        nc.vector.memset(b1_rows[:], 0.0)
         nc.vector.memset(w2_planes[:].bitcast(I32), 0)
         make_identity(nc, ident[:])
 
         def load_w1(e):
             nc.sync.dma_start(
-                out=w1_codes[:, e, :].bitcast(I32),
+                out=w1_raw[:, e, :].bitcast(I32),
                 in_=W1_words[e].rearrange("p n t -> p (n t)").bitcast(I32),
             )
 
-        def load_scale_rows(planes, scales):
+        def load_w1_scales(g):
             for q in range(4):
                 nc.sync.dma_start(
-                    out=planes[32 * q : 32 * q + 4, :, :].bitcast(I32),
-                    in_=scales[:, 4 * q : 4 * q + 4, :].rearrange("g r n -> r g n").bitcast(I32),
+                    out=w1_raw_planes[32 * q : 32 * q + 4 * PLANES, g, :].bitcast(I32),
+                    in_=W1_scales[g * PLANES : (g + 1) * PLANES, 4 * q : 4 * q + 4, :].bitcast(I32),
+                )
+
+        def load_w2_scales():
+            for q in range(4):
+                nc.sync.dma_start(
+                    out=w2_planes[32 * q : 32 * q + 4, :, :].bitcast(I32),
+                    in_=W2_scales[:, 4 * q : 4 * q + 4, :].rearrange("g r n -> r g n").bitcast(I32),
                 )
 
         x_rows = x.rearrange("(p i) k -> p i k", i=ROW_TILES)
-        for i in range(ROW_TILES):
-            nc.sync.dma_start(out=x_sb[:, i, :], in_=x_rows[:, i, :])
+        for i in range(0, ROW_TILES, 2):
+            nc.sync.dma_start(out=x_sb[:, i : i + 2, :], in_=x_rows[:, i : i + 2, :])
         load_w1(0)
-        load_scale_rows(w1_planes, W1_scales)
+        load_w1_scales(0)
+        nc.sync.dma_start(out=b1_rows[:E, :], in_=b1)
         load_w1(1)
-        load_scale_rows(w2_planes, W2_scales)
+        load_w2_scales()
         nc.sync.dma_start(
             out=w2_codes[:].bitcast(I32),
             in_=W2_words.rearrange("g p n t -> p g (n t)").bitcast(I32),
         )
+        nc.sync.dma_start(
+            out=b2_rows[:].rearrange("p e l -> p (e l)"),
+            in_=b2.rearrange("e l -> (e l)").partition_broadcast(P),
+        )
         for e in range(2, E):
+            if e % PLANES == 2 and e // PLANES + 1 < E // PLANES:
+                load_w1_scales(e // PLANES + 1)
             load_w1(e)
 
         for j, src in enumerate((noise_pre, noise, clean_logits)):
             nc.scalar.dma_start(out=gate_in[:, j], in_=src.rearrange("(p i) e -> p i e", i=ROW_TILES))
-        b1_flat = b1.rearrange("e n -> (e n)")
+        nc.scalar.activation(out=warm[:], in_=ones[:], func=ACT.Ln)
 
-        def load_b1(g):
-            nc.scalar.dma_start(
-                out=b1_rows[:, g * GROUP : (g + 1) * GROUP, :].rearrange("p e n -> p (e n)"),
-                in_=b1_flat[g * GROUP * H : (g + 1) * GROUP * H].partition_broadcast(P),
-            )
-
-        load_b1(0)
-        nc.scalar.dma_start(
-            out=b2_rows[:].rearrange("p e l -> p (e l)"),
-            in_=b2.rearrange("e l -> (e l)").partition_broadcast(P),
-        )
-        for g in range(1, E // GROUP):
-            load_b1(g)
+        def flip(rows):
+            flipped = z_banks.tile([P, 2, P], F32, tag="z")
+            for u in range(2):
+                nc.tensor.transpose(flipped[:, u, :], rows.bitcast(F32)[:, u : D // 2 : 2], ident[:])
+            return flipped
 
         x_words = x_grouped[:].bitcast(F32).rearrange("q (i b u) -> q i b u", i=ROW_TILES, u=2)
         for i in range(ROW_TILES):
             rows = slice(i * P, (i + 1) * P)
-            xt = t_banks.tile([P, 2, P], F32, tag="flipped")
-            for u in range(2):
-                nc.tensor.transpose(xt[:, u, :], x_sb[:, i, :].bitcast(F32)[:, u : D // 2 : 2], ident[:])
+            xt = flip(x_sb[:, i, :])
             nc.vector.tensor_copy(out=x_words[:, i], in_=xt[:].rearrange("q u b -> q b u"))
             nc.vector.quantize_mx(
                 out=x_codes[:, rows].bitcast(FP8X4),
                 scales=x_plane[:, rows],
                 in_=x_grouped[:, i * P * PACK : (i + 1) * P * PACK],
             )
+        bt = flip(b1_rows[:])
+        nc.vector.tensor_copy(
+            out=b1_cols[:].rearrange("q e t -> q (e t)").bitcast(F32).rearrange("q (e u) -> q e u", u=2),
+            in_=bt[:, :, :E].rearrange("q u e -> q e u"),
+        )
+
+        w1_codes = {}
+
+        def sort_w1(e):
+            codes = acts.tile([P, H], U32, align_bytes=64)
+            nc.vector.tensor_copy(
+                out=codes[:].bitcast(I32).rearrange("p (t m) -> p t m", t=PACK),
+                in_=w1_raw[:, e, :].bitcast(I32).rearrange("p (m t) -> p t m", t=PACK),
+            )
+            w1_codes[e] = codes
+
+        def sort_w1_scales(g):
+            nc.vector.tensor_copy(
+                out=w1_planes[:, g, :].rearrange("p (t m) -> p t m", t=PACK),
+                in_=w1_raw_planes[:, g, :].rearrange("p (m t) -> p t m", t=PACK),
+            )
+
+        sort_w1(0)
+        sort_w1_scales(0)
 
         shape = [P, ROW_TILES, E]
         pre, noi, cln = gate_in[:, 0], gate_in[:, 1], gate_in[:, 2]
@@ -169,45 +200,37 @@ def tile_mblfe_pa_e_kernel(
             nc.vector.tensor_tensor(out=gates[:], in0=kept[:], in1=over_experts(kinv), op=ALU.mult)
 
         out_rows = out.rearrange("(p i) e l -> p i e l", i=ROW_TILES)
-        biased = {}
-        grouped = {}
-        packed = {}
-        products = {}
+        sums, hidden, grouped, packed, products, biased = {}, {}, {}, {}, {}, {}
 
-        def first_product(e, tiles):
-            for i in tiles:
-                rows = slice(i * P, (i + 1) * P)
-                z = z_banks.tile([P, H], F32)
+        def first_product(e, slots):
+            k = PACK * (e % PLANES)
+            for t in slots:
+                cols = slice(t * P, (t + 1) * P)
+                z = z_banks.tile([P, B], F32, tag="z")
                 nc.tensor.matmul_mx(
                     out=z[:],
-                    lhsT=x_codes[:, rows].bitcast(FP8X4),
-                    lhsT_scale=x_plane[:, rows],
-                    rhs=w1_codes[:, e, :].bitcast(FP8X4),
-                    rhs_scale=w1_planes[:, e, :],
+                    lhsT=w1_codes[e][:, cols].bitcast(FP8X4),
+                    lhsT_scale=w1_planes[k:, e // PLANES, cols],
+                    rhs=x_codes[:].bitcast(FP8X4),
+                    rhs_scale=x_plane[:],
                     start=True,
                     stop=True,
                 )
-                zb = sums.tile([P, PACK, P], F32)
-                nc.vector.tensor_tensor(
-                    out=zb[:],
-                    in0=z[:].rearrange("b (q t) -> b t q", t=PACK),
-                    in1=b1_rows[:, e, :].rearrange("b (q t) -> b t q", t=PACK),
-                    op=ALU.add,
-                )
-                biased[(e, i)] = zb
+                sums[(e, t)] = z
 
-        def flip_and_tanh(e, tiles):
-            if e not in grouped:
-                hg = acts.tile([P, ROW_TILES, P, PACK], BF16, align_bytes=64)
-                grouped[e] = hg
-            hg = grouped[e]
-            for i in tiles:
-                zt = t_banks.tile([P, 512], F32, tag="flipped")
-                for t in range(PACK):
-                    nc.tensor.transpose(zt[:, t * P : (t + 1) * P], biased[(e, i)][:, t, :], ident[:])
+        def add_bias_and_tanh(e, slots):
+            if e not in hidden:
+                ht = acts.tile([P, PACK, B], BF16)
+                hidden[e] = ht
+            for t in slots:
                 nc.scalar.activation(
-                    out=hg[:, i], in_=zt[:].rearrange("q (t b) -> q b t", t=PACK), func=ACT.Tanh
+                    out=hidden[e][:, t, :], in_=sums[(e, t)][:], func=ACT.Tanh, bias=b1_cols[:, e, t : t + 1]
                 )
+
+        def group_hidden(e):
+            hg = acts.tile([P, B, PACK], BF16, align_bytes=64)
+            nc.vector.tensor_copy(out=hg[:], in_=hidden[e][:].rearrange("q t b -> q b t"))
+            grouped[e] = hg
 
         def quantise_hidden(e):
             h_codes = acts.tile([P, B], U32, align_bytes=64)
@@ -215,7 +238,7 @@ def tile_mblfe_pa_e_kernel(
             nc.vector.quantize_mx(
                 out=h_codes[:].bitcast(FP8X4),
                 scales=h_plane[:],
-                in_=grouped[e][:].rearrange("q i b t -> q (i b t)"),
+                in_=grouped[e][:].rearrange("q b t -> q (b t)"),
             )
             packed[e] = (h_codes, h_plane)
 
@@ -233,20 +256,23 @@ def tile_mblfe_pa_e_kernel(
                     start=True,
                     stop=True,
                 )
+            products[e] = y
+
+        def add_b2(e):
             yb = acts.tile([P, ROW_TILES, L], F32)
             nc.vector.tensor_tensor(
                 out=yb[:],
-                in0=y[:],
+                in0=products[e][:],
                 in1=b2_rows[:, e, :].unsqueeze(1).to_broadcast([P, ROW_TILES, L]),
                 op=ALU.add,
             )
-            products[e] = yb
+            biased[e] = yb
 
         def weigh_and_store(e):
             for i in range(ROW_TILES):
                 nc.scalar.activation(
                     out=result[:, i, e, :],
-                    in_=products[e][:, i, :],
+                    in_=biased[e][:, i, :],
                     func=ACT.Copy,
                     scale=gates[:, i, e : e + 1],
                 )
@@ -254,18 +280,28 @@ def tile_mblfe_pa_e_kernel(
                 es = slice(e + 1 - STORE, e + 1)
                 nc.sync.dma_start(out=out_rows[:, :, es, :], in_=result[:, :, es, :])
 
-        for step in range(E + 4):
-            for first in range(0, ROW_TILES, RUN):
-                tiles = range(first, first + RUN)
-                if step < E:
-                    first_product(step, tiles)
-                if 0 <= step - 1 < E:
-                    flip_and_tanh(step - 1, tiles)
-            if step == 0:
+        for s in range(E + 4):
+            if s < E:
+                first_product(s, (0, 1))
+            if 0 <= s - 1 < E:
+                add_bias_and_tanh(s - 1, (0, 1))
+            if 0 <= s - 3 < E:
+                second_product(s - 3)
+            if s < E:
+                first_product(s, (2, 3))
+            if 0 <= s - 1 < E:
+                add_bias_and_tanh(s - 1, (2, 3))
+            if s + 1 < E:
+                if (s + 1) % PLANES == 0:
+                    sort_w1_scales((s + 1) // PLANES)
+                sort_w1(s + 1)
+            if s == 0:
                 finish_gates()
-            if 0 <= step - 4 < E:
-                weigh_and_store(step - 4)
-            if 0 <= step - 2 < E:
-                quantise_hidden(step - 2)
-            if 0 <= step - 3 < E:
-                second_product(step - 3)
+            if 0 <= s - 2 < E:
+                group_hidden(s - 2)
+            if 0 <= s - 3 < E:
+                add_b2(s - 3)
+            if 0 <= s - 2 < E:
+                quantise_hidden(s - 2)
+            if 0 <= s - 4 < E:
+                weigh_and_store(s - 4)

@@ -21,6 +21,7 @@ NOISE_EPS = 0.01
 MEAN_EPS = 1e-8
 PLANES = 4
 STORE = 2
+RUN = 4
 
 FLOPS = 2 * E * B * D * H + 2 * E * B * H * L
 
@@ -229,7 +230,10 @@ def tile_mblfe_pa_e_kernel(
 
         def group_hidden(e):
             hg = acts.tile([P, B, PACK], BF16, align_bytes=64)
-            nc.vector.tensor_copy(out=hg[:], in_=hidden[e][:].rearrange("q t b -> q b t"))
+            nc.vector.tensor_copy(
+                out=hg[:].rearrange("q (c i) t -> q c t i", i=RUN),
+                in_=hidden[e][:].rearrange("q t (c i) -> q c t i", i=RUN),
+            )
             grouped[e] = hg
 
         def quantise_hidden(e):

@@ -33,6 +33,7 @@ def tile_mblfe_pa_e_kernel(
     with ExitStack() as ctx:
         keep = ctx.enter_context(tc.tile_pool(name="keep", bufs=1))
         acts = ctx.enter_context(tc.tile_pool(name="acts", bufs=3))
+        sorted_w1 = ctx.enter_context(tc.tile_pool(name="sorted_w1", bufs=4))
         z_banks = ctx.enter_context(tc.psum_pool(name="z_banks", bufs=6))
         y_banks = ctx.enter_context(tc.psum_pool(name="y_banks", bufs=2))
         ctx.enter_context(tc.manual_schedule())
@@ -56,8 +57,8 @@ def tile_mblfe_pa_e_kernel(
         warm = keep.tile([P, 1], F32)
 
         nc.vector.memset(w1_raw_planes[:].bitcast(I32), 0)
-        nc.vector.memset(ones[:], 1.0)
-        nc.vector.memset(b1_rows[:], 0.0)
+        nc.gpsimd.memset(ones[:], 1.0)
+        nc.gpsimd.memset(b1_rows[:].bitcast(F32), 0.0)
         nc.vector.memset(w2_planes[:].bitcast(I32), 0)
         make_identity(nc, ident[:])
 
@@ -86,8 +87,8 @@ def tile_mblfe_pa_e_kernel(
             nc.sync.dma_start(out=x_sb[:, i : i + 2, :], in_=x_rows[:, i : i + 2, :])
         load_w1(0)
         load_w1_scales(0)
-        nc.sync.dma_start(out=b1_rows[:E, :], in_=b1)
         load_w1(1)
+        load_w1(2)
         load_w2_scales()
         nc.sync.dma_start(
             out=w2_codes[:].bitcast(I32),
@@ -97,14 +98,15 @@ def tile_mblfe_pa_e_kernel(
             out=b2_rows[:].rearrange("p e l -> p (e l)"),
             in_=b2.rearrange("e l -> (e l)").partition_broadcast(P),
         )
-        for e in range(2, E):
-            if e % PLANES == 2 and e // PLANES + 1 < E // PLANES:
+        for e in range(3, E):
+            if e % PLANES == 3 and e // PLANES + 1 < E // PLANES:
                 load_w1_scales(e // PLANES + 1)
             load_w1(e)
 
+        nc.scalar.dma_start(out=b1_rows[:E, :], in_=b1)
         for j, src in enumerate((noise_pre, noise, clean_logits)):
             nc.scalar.dma_start(out=gate_in[:, j], in_=src.rearrange("(p i) e -> p i e", i=ROW_TILES))
-        nc.scalar.activation(out=warm[:], in_=ones[:], func=ACT.Ln)
+        nc.scalar.activation(out=warm[:], in_=ones[:], func=ACT.Exp)
 
         def flip(rows):
             flipped = z_banks.tile([P, 2, P], F32, tag="z")
@@ -113,25 +115,30 @@ def tile_mblfe_pa_e_kernel(
             return flipped
 
         x_words = x_grouped[:].bitcast(F32).rearrange("q (i b u) -> q i b u", i=ROW_TILES, u=2)
-        for i in range(ROW_TILES):
-            rows = slice(i * P, (i + 1) * P)
+
+        def group_x(i):
             xt = flip(x_sb[:, i, :])
             nc.vector.tensor_copy(out=x_words[:, i], in_=xt[:].rearrange("q u b -> q b u"))
+
+        def quantise_x(i):
+            rows = slice(i * P, (i + 1) * P)
             nc.vector.quantize_mx(
                 out=x_codes[:, rows].bitcast(FP8X4),
                 scales=x_plane[:, rows],
                 in_=x_grouped[:, i * P * PACK : (i + 1) * P * PACK],
             )
-        bt = flip(b1_rows[:])
-        nc.vector.tensor_copy(
-            out=b1_cols[:].rearrange("q e t -> q (e t)").bitcast(F32).rearrange("q (e u) -> q e u", u=2),
-            in_=bt[:, :, :E].rearrange("q u e -> q e u"),
-        )
+
+        def group_b1():
+            bt = flip(b1_rows[:])
+            nc.vector.tensor_copy(
+                out=b1_cols[:].rearrange("q e t -> q (e t)").bitcast(F32).rearrange("q (e u) -> q e u", u=2),
+                in_=bt[:, :, :E].rearrange("q u e -> q e u"),
+            )
 
         w1_codes = {}
 
         def sort_w1(e):
-            codes = acts.tile([P, H], U32, align_bytes=64)
+            codes = sorted_w1.tile([P, H], U32, align_bytes=64)
             nc.vector.tensor_copy(
                 out=codes[:].bitcast(I32).rearrange("p (t m) -> p t m", t=PACK),
                 in_=w1_raw[:, e, :].bitcast(I32).rearrange("p (m t) -> p t m", t=PACK),
@@ -144,8 +151,6 @@ def tile_mblfe_pa_e_kernel(
                 in_=w1_raw_planes[:, g, :].rearrange("p (m t) -> p t m", t=PACK),
             )
 
-        sort_w1(0)
-        sort_w1_scales(0)
 
         shape = [P, ROW_TILES, E]
         pre, noi, cln = gate_in[:, 0], gate_in[:, 1], gate_in[:, 2]
@@ -155,101 +160,139 @@ def tile_mblfe_pa_e_kernel(
         nc.scalar.activation(out=decay[:], in_=mag[:], func=ACT.Exp, scale=-1.0)
         log1p = keep.tile(shape, F32)
         nc.scalar.activation(out=log1p[:], in_=decay[:], func=ACT.Ln, bias=1.0)
-        softplus = keep.tile(shape, F32)
-        nc.vector.scalar_tensor_tensor(
-            out=softplus[:], in0=pre, scalar=0.0, in1=log1p[:], op0=ALU.max, op1=ALU.add
-        )
-        noisy = keep.tile(shape, F32)
-        nc.vector.scalar_tensor_tensor(
-            out=noisy[:], in0=softplus[:], scalar=NOISE_EPS, in1=noi, op0=ALU.add, op1=ALU.mult
-        )
-        logits = keep.tile(shape, F32)
-        nc.vector.tensor_tensor(out=logits[:], in0=noisy[:], in1=cln, op=ALU.add)
+        nc.scalar.activation(out=warm[:], in_=ones[:], func=ACT.Tanh)
 
         def over_experts(per_row):
             return per_row[:].unsqueeze(2).to_broadcast(shape)
 
+        softplus = keep.tile(shape, F32)
+        noisy = keep.tile(shape, F32)
+        logits = keep.tile(shape, F32)
         top = keep.tile([P, ROW_TILES], F32)
-        nc.vector.tensor_reduce(out=top[:], in_=logits[:], axis=AX.X, op=ALU.max)
         shifted = keep.tile(shape, F32)
-        nc.vector.tensor_tensor(out=shifted[:], in0=logits[:], in1=over_experts(top), op=ALU.subtract)
         expd = keep.tile(shape, F32)
-        nc.scalar.activation(out=expd[:], in_=shifted[:], func=ACT.Exp)
+        esum = keep.tile([P, ROW_TILES], F32)
+        einv = keep.tile([P, ROW_TILES], F32)
+        prob = keep.tile(shape, F32)
+        psum_row = keep.tile([P, ROW_TILES], F32)
+        cut = keep.tile([P, ROW_TILES], F32)
+        alive = keep.tile(shape, F32)
+        kept = keep.tile(shape, F32)
+        ksum = keep.tile([P, ROW_TILES], F32)
+        kinv = keep.tile([P, ROW_TILES], F32)
         gates = keep.tile(shape, F32)
-
-        def finish_gates():
-            esum = keep.tile([P, ROW_TILES], F32)
-            nc.vector.tensor_reduce(out=esum[:], in_=expd[:], axis=AX.X, op=ALU.add)
-            einv = keep.tile([P, ROW_TILES], F32)
-            nc.vector.reciprocal(out=einv[:], in_=esum[:])
-            prob = keep.tile(shape, F32)
-            nc.vector.tensor_tensor(out=prob[:], in0=expd[:], in1=over_experts(einv), op=ALU.mult)
-            psum_row = keep.tile([P, ROW_TILES], F32)
-            nc.vector.tensor_reduce(out=psum_row[:], in_=prob[:], axis=AX.X, op=ALU.add)
-            cut = keep.tile([P, ROW_TILES], F32)
-            nc.vector.tensor_scalar(
+        vec = nc.vector
+        logit_steps = [
+            lambda: vec.scalar_tensor_tensor(
+                out=softplus[:], in0=pre, scalar=0.0, in1=log1p[:], op0=ALU.max, op1=ALU.add
+            ),
+            lambda: vec.scalar_tensor_tensor(
+                out=noisy[:], in0=softplus[:], scalar=NOISE_EPS, in1=noi, op0=ALU.add, op1=ALU.mult
+            ),
+            lambda: vec.tensor_tensor(out=logits[:], in0=noisy[:], in1=cln, op=ALU.add),
+            lambda: vec.tensor_reduce(out=top[:], in_=logits[:], axis=AX.X, op=ALU.max),
+            lambda: vec.tensor_tensor(
+                out=shifted[:], in0=logits[:], in1=over_experts(top), op=ALU.subtract
+            ),
+        ]
+        gate_steps = [
+            lambda: vec.tensor_reduce(out=esum[:], in_=expd[:], axis=AX.X, op=ALU.add),
+            lambda: vec.reciprocal(out=einv[:], in_=esum[:]),
+            lambda: vec.tensor_tensor(out=prob[:], in0=expd[:], in1=over_experts(einv), op=ALU.mult),
+            lambda: vec.tensor_reduce(out=psum_row[:], in_=prob[:], axis=AX.X, op=ALU.add),
+            lambda: vec.tensor_scalar(
                 out=cut[:], in0=psum_row[:], scalar1=1.0 / E, scalar2=-MEAN_EPS, op0=ALU.mult, op1=ALU.add
-            )
-            alive = keep.tile(shape, F32)
-            nc.vector.tensor_tensor(out=alive[:], in0=prob[:], in1=over_experts(cut), op=ALU.is_ge)
-            kept = keep.tile(shape, F32)
-            nc.vector.tensor_tensor(out=kept[:], in0=prob[:], in1=alive[:], op=ALU.mult)
-            ksum = keep.tile([P, ROW_TILES], F32)
-            nc.vector.tensor_reduce(out=ksum[:], in_=kept[:], axis=AX.X, op=ALU.add)
-            kinv = keep.tile([P, ROW_TILES], F32)
-            nc.vector.reciprocal(out=kinv[:], in_=ksum[:])
-            nc.vector.tensor_tensor(out=gates[:], in0=kept[:], in1=over_experts(kinv), op=ALU.mult)
+            ),
+            lambda: vec.tensor_tensor(out=alive[:], in0=prob[:], in1=over_experts(cut), op=ALU.is_ge),
+            lambda: vec.tensor_tensor(out=kept[:], in0=prob[:], in1=alive[:], op=ALU.mult),
+            lambda: vec.tensor_reduce(out=ksum[:], in_=kept[:], axis=AX.X, op=ALU.add),
+            lambda: vec.reciprocal(out=kinv[:], in_=ksum[:]),
+            lambda: vec.tensor_tensor(out=gates[:], in0=kept[:], in1=over_experts(kinv), op=ALU.mult),
+        ]
+
+        def next_gate_step():
+            if gate_steps:
+                step = gate_steps[0]
+                gate_steps.remove(step)
+                step()
+
+        group_x(0)
+        group_x(1)
+        quantise_x(0)
+        sort_w1_scales(0)
+        quantise_x(1)
+        group_b1()
+        sort_w1(0)
+        group_x(2)
+        group_x(3)
+        quantise_x(2)
+        logit_steps[0]()
+        quantise_x(3)
+        logit_steps[1]()
+        sort_w1(1)
+        for logit_step in logit_steps[2:]:
+            logit_step()
 
         out_rows = out.rearrange("(p i) e l -> p i e l", i=ROW_TILES)
+        half = ROW_TILES // 2
+        pieces = [(0, 0, half), (0, half, half)]
+        pieces += [(e, 0, ROW_TILES) for e in range(1, E - 1)]
+        pieces += [(E - 1, 0, half), (E - 1, half, half)]
         sums, hidden, grouped, packed, products, biased = {}, {}, {}, {}, {}, {}
 
-        def first_product(e, slots):
+        def first_product(s, slots):
+            e, i0, n = pieces[s]
             k = PACK * (e % PLANES)
+            rows = slice(i0 * P, (i0 + n) * P)
             for t in slots:
                 cols = slice(t * P, (t + 1) * P)
-                z = z_banks.tile([P, B], F32, tag="z")
+                z = z_banks.tile([P, n * P], F32, tag="z")
                 nc.tensor.matmul_mx(
                     out=z[:],
                     lhsT=w1_codes[e][:, cols].bitcast(FP8X4),
                     lhsT_scale=w1_planes[k:, e // PLANES, cols],
-                    rhs=x_codes[:].bitcast(FP8X4),
-                    rhs_scale=x_plane[:],
+                    rhs=x_codes[:, rows].bitcast(FP8X4),
+                    rhs_scale=x_plane[:, rows],
                     start=True,
                     stop=True,
                 )
-                sums[(e, t)] = z
+                sums[(s, t)] = z
 
-        def add_bias_and_tanh(e, slots):
-            if e not in hidden:
-                ht = acts.tile([P, PACK, B], BF16)
-                hidden[e] = ht
+        def add_bias_and_tanh(s, slots):
+            e, i0, n = pieces[s]
+            if s not in hidden:
+                ht = acts.tile([P, PACK, n * P], BF16)
+                hidden[s] = ht
             for t in slots:
                 nc.scalar.activation(
-                    out=hidden[e][:, t, :], in_=sums[(e, t)][:], func=ACT.Tanh, bias=b1_cols[:, e, t : t + 1]
+                    out=hidden[s][:, t, :], in_=sums[(s, t)][:], func=ACT.Tanh, bias=b1_cols[:, e, t : t + 1]
                 )
 
-        def group_hidden(e):
-            hg = acts.tile([P, B, PACK], BF16, align_bytes=64)
+        def group_hidden(s):
+            e, i0, n = pieces[s]
+            hg = acts.tile([P, n * P, PACK], BF16, align_bytes=64)
             nc.vector.tensor_copy(
                 out=hg[:].rearrange("q (c i) t -> q c t i", i=RUN),
-                in_=hidden[e][:].rearrange("q t (c i) -> q c t i", i=RUN),
+                in_=hidden[s][:].rearrange("q t (c i) -> q c t i", i=RUN),
             )
-            grouped[e] = hg
+            grouped[s] = hg
 
-        def quantise_hidden(e):
-            h_codes = acts.tile([P, B], U32, align_bytes=64)
-            h_plane = acts.tile([P, B], U8, align_bytes=64)
+        def quantise_hidden(s):
+            e, i0, n = pieces[s]
+            h_codes = acts.tile([P, n * P], U32, align_bytes=64)
+            h_plane = acts.tile([P, n * P], U8, align_bytes=64)
             nc.vector.quantize_mx(
                 out=h_codes[:].bitcast(FP8X4),
                 scales=h_plane[:],
-                in_=grouped[e][:].rearrange("q b t -> q (b t)"),
+                in_=grouped[s][:].rearrange("q b t -> q (b t)"),
             )
-            packed[e] = (h_codes, h_plane)
+            packed[s] = (h_codes, h_plane)
 
-        def second_product(e):
-            h_codes, h_plane = packed[e]
-            y = y_banks.tile([P, ROW_TILES, L], F32)
-            for i in range(ROW_TILES):
+        def second_product(s):
+            e, i0, n = pieces[s]
+            h_codes, h_plane = packed[s]
+            y = y_banks.tile([P, n, L], F32)
+            for i in range(n):
                 rows = slice(i * P, (i + 1) * P)
                 nc.tensor.matmul_mx(
                     out=y[:, i, :],
@@ -260,52 +303,68 @@ def tile_mblfe_pa_e_kernel(
                     start=True,
                     stop=True,
                 )
-            products[e] = y
+            products[s] = y
 
-        def add_b2(e):
-            yb = acts.tile([P, ROW_TILES, L], F32)
+        def add_b2(s):
+            e, i0, n = pieces[s]
+            yb = acts.tile([P, n, L], F32)
             nc.vector.tensor_tensor(
                 out=yb[:],
-                in0=products[e][:],
-                in1=b2_rows[:, e, :].unsqueeze(1).to_broadcast([P, ROW_TILES, L]),
+                in0=products[s][:],
+                in1=b2_rows[:, e, :].unsqueeze(1).to_broadcast([P, n, L]),
                 op=ALU.add,
             )
-            biased[e] = yb
+            biased[s] = yb
 
-        def weigh_and_store(e):
-            for i in range(ROW_TILES):
+        def store(tiles, experts):
+            nc.sync.dma_start(out=out_rows[:, tiles, experts, :], in_=result[:, tiles, experts, :])
+
+        def weigh_and_store(s):
+            e, i0, n = pieces[s]
+            for i in range(n):
                 nc.scalar.activation(
-                    out=result[:, i, e, :],
-                    in_=biased[e][:, i, :],
+                    out=result[:, i0 + i, e, :],
+                    in_=biased[s][:, i, :],
                     func=ACT.Copy,
-                    scale=gates[:, i, e : e + 1],
+                    scale=gates[:, i0 + i, e : e + 1],
                 )
-            if e % STORE == STORE - 1:
-                es = slice(e + 1 - STORE, e + 1)
-                nc.sync.dma_start(out=out_rows[:, :, es, :], in_=result[:, :, es, :])
+            if e >= E - STORE:
+                store(slice(i0, i0 + n), slice(e, e + 1))
+            elif e % STORE == STORE - 1:
+                store(slice(0, ROW_TILES), slice(e + 1 - STORE, e + 1))
 
-        for s in range(E + 4):
-            if s < E:
+        def sort_next(s):
+            e, i0, n = pieces[s]
+            if i0 == 0 and e + 2 < E:
+                if (e + 2) % PLANES == 0:
+                    sort_w1_scales((e + 2) // PLANES)
+                sort_w1(e + 2)
+
+        for s in range(len(pieces) + 4):
+            if s < len(pieces):
                 first_product(s, (0, 1))
-            if 0 <= s - 1 < E:
+            if 0 <= s - 1 < len(pieces):
                 add_bias_and_tanh(s - 1, (0, 1))
-            if 0 <= s - 3 < E:
+            if 0 <= s - 3 < len(pieces):
                 second_product(s - 3)
-            if s < E:
+            if s < len(pieces):
                 first_product(s, (2, 3))
-            if 0 <= s - 1 < E:
+            if 0 <= s - 1 < len(pieces):
                 add_bias_and_tanh(s - 1, (2, 3))
-            if s + 1 < E:
-                if (s + 1) % PLANES == 0:
-                    sort_w1_scales((s + 1) // PLANES)
-                sort_w1(s + 1)
-            if s == 0:
-                finish_gates()
-            if 0 <= s - 2 < E:
+            if s == 1:
+                nc.scalar.activation(out=expd[:], in_=shifted[:], func=ACT.Exp)
+            if s < len(pieces):
+                sort_next(s)
+            if s >= 2:
+                next_gate_step()
+            if 0 <= s - 2 < len(pieces):
                 group_hidden(s - 2)
-            if 0 <= s - 3 < E:
+                next_gate_step()
+            if 0 <= s - 3 < len(pieces):
                 add_b2(s - 3)
-            if 0 <= s - 2 < E:
+                next_gate_step()
+            if 0 <= s - 2 < len(pieces):
                 quantise_hidden(s - 2)
-            if 0 <= s - 4 < E:
+                next_gate_step()
+            if 0 <= s - 4 < len(pieces):
                 weigh_and_store(s - 4)

@@ -49,17 +49,19 @@ def tile_mblfe_pa_e_kernel(
         w2_planes = keep.tile([P, E, L], U8, align_bytes=64)
         b1_rows = keep.tile([P, H], BF16)
         b1_cols = keep.tile([P, E, PACK], BF16)
-        b2_rows = keep.tile([P, E, L], BF16)
+        b2_flat = keep.tile([P, E * L], BF16)
+        b2_rows = keep.tile([P, E * L], BF16)
+        spread = keep.tile([P, P], BF16)
         gate_in = keep.tile([P, 3, ROW_TILES, E], BF16)
         result = keep.tile([P, ROW_TILES, E, L], F32)
         ident = keep.tile([P, P], F32)
         ones = keep.tile([P, 1], F32)
         warm = keep.tile([P, 1], F32)
 
+        nc.vector.memset(b1_rows[:].bitcast(F32), 0.0)
         nc.vector.memset(w1_raw_planes[:].bitcast(I32), 0)
-        nc.gpsimd.memset(ones[:], 1.0)
-        nc.gpsimd.memset(b1_rows[:].bitcast(F32), 0.0)
         nc.vector.memset(w2_planes[:].bitcast(I32), 0)
+        nc.gpsimd.memset(ones[:], 1.0)
         make_identity(nc, ident[:])
 
         def load_w1(e):
@@ -82,31 +84,39 @@ def tile_mblfe_pa_e_kernel(
                     in_=W2_scales[:, 4 * q : 4 * q + 4, :].rearrange("g r n -> r g n").bitcast(I32),
                 )
 
+        def load_w2(g):
+            es = slice(g * PLANES, (g + 1) * PLANES)
+            nc.sync.dma_start(
+                out=w2_codes[:, es, :].bitcast(I32),
+                in_=W2_words[es].rearrange("g p n t -> p g (n t)").bitcast(I32),
+            )
+
+        def load_gate_input(queue, j, src):
+            queue.dma_start(out=gate_in[:, j], in_=src.rearrange("(p i) e -> p i e", i=ROW_TILES))
+
+        load_gate_input(nc.scalar, 0, noise_pre)
+        nc.scalar.dma_start(out=b1_rows[:E, :], in_=b1)
         x_rows = x.rearrange("(p i) k -> p i k", i=ROW_TILES)
         for i in range(0, ROW_TILES, 2):
             nc.sync.dma_start(out=x_sb[:, i : i + 2, :], in_=x_rows[:, i : i + 2, :])
         load_w1(0)
         load_w1_scales(0)
-        load_w1(1)
-        load_w1(2)
-        load_w2_scales()
-        nc.sync.dma_start(
-            out=w2_codes[:].bitcast(I32),
-            in_=W2_words.rearrange("g p n t -> p g (n t)").bitcast(I32),
-        )
-        nc.sync.dma_start(
-            out=b2_rows[:].rearrange("p e l -> p (e l)"),
-            in_=b2.rearrange("e l -> (e l)").partition_broadcast(P),
-        )
-        for e in range(3, E):
-            if e % PLANES == 3 and e // PLANES + 1 < E // PLANES:
-                load_w1_scales(e // PLANES + 1)
-            load_w1(e)
-
-        nc.scalar.dma_start(out=b1_rows[:E, :], in_=b1)
-        for j, src in enumerate((noise_pre, noise, clean_logits)):
-            nc.scalar.dma_start(out=gate_in[:, j], in_=src.rearrange("(p i) e -> p i e", i=ROW_TILES))
         nc.scalar.activation(out=warm[:], in_=ones[:], func=ACT.Exp)
+        load_gate_input(nc.gpsimd, 1, noise)
+        load_gate_input(nc.gpsimd, 2, clean_logits)
+        nc.gpsimd.memset(b2_flat[:].bitcast(F32), 0.0)
+        nc.gpsimd.memset(spread[:], 1.0)
+        nc.gpsimd.dma_start(out=b2_flat[:1, :], in_=b2.rearrange("(o e) l -> o (e l)", o=1))
+        for e in range(1, PLANES):
+            load_w1(e)
+        load_w2(0)
+        load_w2_scales()
+        for g in range(1, E // PLANES):
+            load_w1_scales(g)
+        for g in range(1, E // PLANES):
+            for e in range(g * PLANES, (g + 1) * PLANES):
+                load_w1(e)
+            load_w2(g)
 
         def flip(rows):
             flipped = z_banks.tile([P, 2, P], F32, tag="z")
@@ -172,9 +182,6 @@ def tile_mblfe_pa_e_kernel(
         shifted = keep.tile(shape, F32)
         expd = keep.tile(shape, F32)
         esum = keep.tile([P, ROW_TILES], F32)
-        einv = keep.tile([P, ROW_TILES], F32)
-        prob = keep.tile(shape, F32)
-        psum_row = keep.tile([P, ROW_TILES], F32)
         cut = keep.tile([P, ROW_TILES], F32)
         alive = keep.tile(shape, F32)
         kept = keep.tile(shape, F32)
@@ -197,14 +204,11 @@ def tile_mblfe_pa_e_kernel(
         ]
         gate_steps = [
             lambda: vec.tensor_reduce(out=esum[:], in_=expd[:], axis=AX.X, op=ALU.add),
-            lambda: vec.reciprocal(out=einv[:], in_=esum[:]),
-            lambda: vec.tensor_tensor(out=prob[:], in0=expd[:], in1=over_experts(einv), op=ALU.mult),
-            lambda: vec.tensor_reduce(out=psum_row[:], in_=prob[:], axis=AX.X, op=ALU.add),
             lambda: vec.tensor_scalar(
-                out=cut[:], in0=psum_row[:], scalar1=1.0 / E, scalar2=-MEAN_EPS, op0=ALU.mult, op1=ALU.add
+                out=cut[:], in0=esum[:], scalar1=1.0 / E - MEAN_EPS, scalar2=None, op0=ALU.mult
             ),
-            lambda: vec.tensor_tensor(out=alive[:], in0=prob[:], in1=over_experts(cut), op=ALU.is_ge),
-            lambda: vec.tensor_tensor(out=kept[:], in0=prob[:], in1=alive[:], op=ALU.mult),
+            lambda: vec.tensor_tensor(out=alive[:], in0=expd[:], in1=over_experts(cut), op=ALU.is_ge),
+            lambda: vec.tensor_tensor(out=kept[:], in0=expd[:], in1=alive[:], op=ALU.mult),
             lambda: vec.tensor_reduce(out=ksum[:], in_=kept[:], axis=AX.X, op=ALU.add),
             lambda: vec.reciprocal(out=kinv[:], in_=ksum[:]),
             lambda: vec.tensor_tensor(out=gates[:], in0=kept[:], in1=over_experts(kinv), op=ALU.mult),
@@ -219,17 +223,17 @@ def tile_mblfe_pa_e_kernel(
         group_x(0)
         group_x(1)
         quantise_x(0)
-        sort_w1_scales(0)
-        quantise_x(1)
-        group_b1()
-        sort_w1(0)
         group_x(2)
+        quantise_x(1)
         group_x(3)
+        sort_w1(0)
         quantise_x(2)
-        logit_steps[0]()
+        group_b1()
         quantise_x(3)
-        logit_steps[1]()
+        sort_w1_scales(0)
+        logit_steps[0]()
         sort_w1(1)
+        logit_steps[1]()
         for logit_step in logit_steps[2:]:
             logit_step()
 
@@ -291,7 +295,7 @@ def tile_mblfe_pa_e_kernel(
         def second_product(s):
             e, i0, n = pieces[s]
             h_codes, h_plane = packed[s]
-            y = y_banks.tile([P, n, L], F32)
+            y = y_banks.tile([P, n, L], F32, tag="y")
             for i in range(n):
                 rows = slice(i * P, (i + 1) * P)
                 nc.tensor.matmul_mx(
@@ -311,10 +315,16 @@ def tile_mblfe_pa_e_kernel(
             nc.vector.tensor_tensor(
                 out=yb[:],
                 in0=products[s][:],
-                in1=b2_rows[:, e, :].unsqueeze(1).to_broadcast([P, n, L]),
+                in1=b2_rows[:, e * L : (e + 1) * L].unsqueeze(1).to_broadcast([P, n, L]),
                 op=ALU.add,
             )
             biased[s] = yb
+
+        def spread_b2(g):
+            cols = slice(g * PLANES * L, (g + 1) * PLANES * L)
+            bank = y_banks.tile([P, PLANES * L], F32, tag="y")
+            nc.tensor.matmul(bank[:], lhsT=spread[:], rhs=b2_flat[:, cols], start=True, stop=True)
+            nc.scalar.copy(b2_rows[:, cols], bank[:])
 
         def store(tiles, experts):
             nc.sync.dma_start(out=out_rows[:, tiles, experts, :], in_=result[:, tiles, experts, :])
@@ -353,6 +363,8 @@ def tile_mblfe_pa_e_kernel(
                 add_bias_and_tanh(s - 1, (2, 3))
             if s == 1:
                 nc.scalar.activation(out=expd[:], in_=shifted[:], func=ACT.Exp)
+            if 1 <= s <= E // PLANES:
+                spread_b2(s - 1)
             if s < len(pieces):
                 sort_next(s)
             if s >= 2:

@@ -21,7 +21,7 @@ NOISE_EPS = 0.01
 MEAN_EPS = 1e-8
 PLANES = 4
 STORE = 2
-RUN = 4
+RUN = 8
 
 FLOPS = 2 * E * B * D * H + 2 * E * B * H * L
 
@@ -110,11 +110,12 @@ def tile_mblfe_pa_e_kernel(
         for e in range(1, PLANES):
             load_w1(e)
         load_w2(0)
+        load_w1(PLANES)
         load_w2_scales()
         for g in range(1, E // PLANES):
             load_w1_scales(g)
         for g in range(1, E // PLANES):
-            for e in range(g * PLANES, (g + 1) * PLANES):
+            for e in range(g * PLANES + 1, min((g + 1) * PLANES + 1, E)):
                 load_w1(e)
             load_w2(g)
 
@@ -346,9 +347,9 @@ def tile_mblfe_pa_e_kernel(
         def sort_next(s):
             e, i0, n = pieces[s]
             if i0 == 0 and e + 2 < E:
-                if (e + 2) % PLANES == 0:
-                    sort_w1_scales((e + 2) // PLANES)
                 sort_w1(e + 2)
+            if i0 == 0 and e % PLANES == PLANES - 1 and e + 1 < E:
+                sort_w1_scales((e + 1) // PLANES)
 
         for s in range(len(pieces) + 4):
             if s < len(pieces):

@@ -21,6 +21,7 @@ NOISE_EPS = 0.01
 MEAN_EPS = 1e-8
 PLANES = 4
 STORE = 2
+VECTOR_EVERY = 4
 RUN = 8
 
 FLOPS = 2 * E * B * D * H + 2 * E * B * H * L
@@ -323,7 +324,7 @@ def tile_mblfe_pa_e_kernel(
 
         def spread_b2(g):
             cols = slice(g * PLANES * L, (g + 1) * PLANES * L)
-            bank = y_banks.tile([P, PLANES * L], F32, tag="y")
+            bank = y_banks.tile([P, PLANES * L], BF16, tag="y")
             nc.tensor.matmul(bank[:], lhsT=spread[:], rhs=b2_flat[:, cols], start=True, stop=True)
             nc.scalar.copy(b2_rows[:, cols], bank[:])
 
@@ -333,12 +334,12 @@ def tile_mblfe_pa_e_kernel(
         def weigh_and_store(s):
             e, i0, n = pieces[s]
             for i in range(n):
-                nc.scalar.activation(
-                    out=result[:, i0 + i, e, :],
-                    in_=biased[s][:, i, :],
-                    func=ACT.Copy,
-                    scale=gates[:, i0 + i, e : e + 1],
-                )
+                weighed = result[:, i0 + i, e, :]
+                gate = gates[:, i0 + i, e : e + 1]
+                if e % VECTOR_EVERY == VECTOR_EVERY - 1 and (e < E - 1 or i % 2 == 0):
+                    nc.vector.tensor_scalar_mul(out=weighed, in0=biased[s][:, i, :], scalar1=gate)
+                else:
+                    nc.scalar.activation(out=weighed, in_=biased[s][:, i, :], func=ACT.Copy, scale=gate)
             if e >= E - STORE:
                 store(slice(i0, i0 + n), slice(e, e + 1))
             elif e % STORE == STORE - 1:

@@ -50,7 +50,7 @@ def tile_mblfe_pa_e_kernel(
         w2_planes = keep.tile([P, E, L], U8, align_bytes=64)
         b1_rows = keep.tile([P, H], BF16)
         b1_cols = keep.tile([P, E, PACK], BF16)
-        b2_flat = keep.tile([P, E * L], BF16)
+        b2_flat = keep.tile([P, PLANES * L], BF16)
         b2_rows = keep.tile([P, E * L], BF16)
         spread = keep.tile([P, P], BF16)
         gate_in = keep.tile([P, 3, ROW_TILES, E], BF16)
@@ -59,10 +59,11 @@ def tile_mblfe_pa_e_kernel(
         ones = keep.tile([P, 1], F32)
         warm = keep.tile([P, 1], F32)
 
+        nc.vector.memset(ones[:], 1.0)
+        nc.vector.memset(w1_raw_planes[:, 0, :].bitcast(I32), 0)
         nc.vector.memset(b1_rows[:].bitcast(F32), 0.0)
-        nc.vector.memset(w1_raw_planes[:].bitcast(I32), 0)
+        nc.vector.memset(w1_raw_planes[:, 1:, :].rearrange("p g n -> p (g n)").bitcast(I32), 0)
         nc.vector.memset(w2_planes[:].bitcast(I32), 0)
-        nc.gpsimd.memset(ones[:], 1.0)
         make_identity(nc, ident[:])
 
         def load_w1(e):
@@ -98,16 +99,20 @@ def tile_mblfe_pa_e_kernel(
         load_gate_input(nc.scalar, 0, noise_pre)
         nc.scalar.dma_start(out=b1_rows[:E, :], in_=b1)
         x_rows = x.rearrange("(p i) k -> p i k", i=ROW_TILES)
-        for i in range(0, ROW_TILES, 2):
+
+        def load_x(i):
             nc.sync.dma_start(out=x_sb[:, i : i + 2, :], in_=x_rows[:, i : i + 2, :])
-        load_w1(0)
+
+        load_x(0)
         load_w1_scales(0)
+        load_w1(0)
+        load_x(2)
         nc.scalar.activation(out=warm[:], in_=ones[:], func=ACT.Exp)
-        load_gate_input(nc.gpsimd, 1, noise)
-        load_gate_input(nc.gpsimd, 2, clean_logits)
+        load_gate_input(nc.scalar, 1, noise)
+        load_gate_input(nc.scalar, 2, clean_logits)
         nc.gpsimd.memset(b2_flat[:].bitcast(F32), 0.0)
         nc.gpsimd.memset(spread[:], 1.0)
-        nc.gpsimd.dma_start(out=b2_flat[:1, :], in_=b2.rearrange("(o e) l -> o (e l)", o=1))
+        nc.gpsimd.dma_start(out=b2_flat[:1, :], in_=b2[:PLANES, :].rearrange("(o e) l -> o (e l)", o=1))
         for e in range(1, PLANES):
             load_w1(e)
         load_w2(0)
@@ -119,6 +124,10 @@ def tile_mblfe_pa_e_kernel(
             for e in range(g * PLANES + 1, min((g + 1) * PLANES + 1, E)):
                 load_w1(e)
             load_w2(g)
+        nc.sync.dma_start(
+            out=b2_rows[:, PLANES * L :],
+            in_=b2[PLANES:, :].rearrange("e l -> (e l)").partition_broadcast(P),
+        )
 
         def flip(rows):
             flipped = z_banks.tile([P, 2, P], F32, tag="z")
@@ -152,8 +161,8 @@ def tile_mblfe_pa_e_kernel(
         def sort_w1(e):
             codes = sorted_w1.tile([P, H], U32, align_bytes=64)
             nc.vector.tensor_copy(
-                out=codes[:].bitcast(I32).rearrange("p (t m) -> p t m", t=PACK),
-                in_=w1_raw[:, e, :].bitcast(I32).rearrange("p (m t) -> p t m", t=PACK),
+                out=codes[:].bitcast(I32).rearrange("p (t c i) -> p c t i", t=PACK, i=PACK),
+                in_=w1_raw[:, e, :].bitcast(I32).rearrange("p (c i t) -> p c t i", t=PACK, i=PACK),
             )
             w1_codes[e] = codes
 
@@ -204,7 +213,7 @@ def tile_mblfe_pa_e_kernel(
                 out=shifted[:], in0=logits[:], in1=over_experts(top), op=ALU.subtract
             ),
         ]
-        gate_steps = [
+        gate_steps = logit_steps[2:] + [
             lambda: vec.tensor_reduce(out=esum[:], in_=expd[:], axis=AX.X, op=ALU.add),
             lambda: vec.tensor_scalar(
                 out=cut[:], in0=esum[:], scalar1=1.0 / E - MEAN_EPS, scalar2=None, op0=ALU.mult
@@ -225,19 +234,17 @@ def tile_mblfe_pa_e_kernel(
         group_x(0)
         group_x(1)
         quantise_x(0)
-        group_x(2)
-        quantise_x(1)
-        group_x(3)
-        sort_w1(0)
-        quantise_x(2)
         group_b1()
-        quantise_x(3)
+        quantise_x(1)
         sort_w1_scales(0)
+        sort_w1(0)
+        group_x(2)
+        group_x(3)
+        quantise_x(2)
         logit_steps[0]()
+        quantise_x(3)
         sort_w1(1)
         logit_steps[1]()
-        for logit_step in logit_steps[2:]:
-            logit_step()
 
         out_rows = out.rearrange("(p i) e l -> p i e l", i=ROW_TILES)
         half = ROW_TILES // 2
@@ -322,11 +329,10 @@ def tile_mblfe_pa_e_kernel(
             )
             biased[s] = yb
 
-        def spread_b2(g):
-            cols = slice(g * PLANES * L, (g + 1) * PLANES * L)
+        def spread_b2():
             bank = y_banks.tile([P, PLANES * L], BF16, tag="y")
-            nc.tensor.matmul(bank[:], lhsT=spread[:], rhs=b2_flat[:, cols], start=True, stop=True)
-            nc.scalar.copy(b2_rows[:, cols], bank[:])
+            nc.tensor.matmul(bank[:], lhsT=spread[:], rhs=b2_flat[:], start=True, stop=True)
+            nc.scalar.copy(b2_rows[:, : PLANES * L], bank[:])
 
         def store(tiles, experts):
             nc.sync.dma_start(out=out_rows[:, tiles, experts, :], in_=result[:, tiles, experts, :])
@@ -355,6 +361,8 @@ def tile_mblfe_pa_e_kernel(
         for s in range(len(pieces) + 4):
             if s < len(pieces):
                 first_product(s, (0, 1))
+            if s == 3:
+                nc.scalar.activation(out=expd[:], in_=shifted[:], func=ACT.Exp)
             if 0 <= s - 1 < len(pieces):
                 add_bias_and_tanh(s - 1, (0, 1))
             if 0 <= s - 3 < len(pieces):
@@ -364,21 +372,20 @@ def tile_mblfe_pa_e_kernel(
             if 0 <= s - 1 < len(pieces):
                 add_bias_and_tanh(s - 1, (2, 3))
             if s == 1:
-                nc.scalar.activation(out=expd[:], in_=shifted[:], func=ACT.Exp)
-            if 1 <= s <= E // PLANES:
-                spread_b2(s - 1)
+                spread_b2()
             if s < len(pieces):
                 sort_next(s)
-            if s >= 2:
                 next_gate_step()
             if 0 <= s - 2 < len(pieces):
                 group_hidden(s - 2)
-                next_gate_step()
+                if s >= 3:
+                    next_gate_step()
             if 0 <= s - 3 < len(pieces):
                 add_b2(s - 3)
                 next_gate_step()
             if 0 <= s - 2 < len(pieces):
                 quantise_hidden(s - 2)
-                next_gate_step()
+                if s >= 3:
+                    next_gate_step()
             if 0 <= s - 4 < len(pieces):
                 weigh_and_store(s - 4)

@@ -21,7 +21,7 @@ NOISE_EPS = 0.01
 MEAN_EPS = 1e-8
 PLANES = 4
 STORE = 2
-VECTOR_EVERY = 4
+VECTOR_EVERY = 3
 RUN = 8
 
 FLOPS = 2 * E * B * D * H + 2 * E * B * H * L
@@ -59,9 +59,9 @@ def tile_mblfe_pa_e_kernel(
         ones = keep.tile([P, 1], F32)
         warm = keep.tile([P, 1], F32)
 
+        nc.vector.memset(b1_rows[:].bitcast(F32), 0.0)
         nc.vector.memset(ones[:], 1.0)
         nc.vector.memset(w1_raw_planes[:, 0, :].bitcast(I32), 0)
-        nc.vector.memset(b1_rows[:].bitcast(F32), 0.0)
         nc.vector.memset(w1_raw_planes[:, 1:, :].rearrange("p g n -> p (g n)").bitcast(I32), 0)
         nc.vector.memset(w2_planes[:].bitcast(I32), 0)
         make_identity(nc, ident[:])
@@ -96,17 +96,12 @@ def tile_mblfe_pa_e_kernel(
         def load_gate_input(queue, j, src):
             queue.dma_start(out=gate_in[:, j], in_=src.rearrange("(p i) e -> p i e", i=ROW_TILES))
 
-        load_gate_input(nc.scalar, 0, noise_pre)
-        nc.scalar.dma_start(out=b1_rows[:E, :], in_=b1)
+        load_gate_input(nc.sync, 0, noise_pre)
+        nc.gpsimd.dma_start(out=b1_rows[:E, :], in_=b1)
         x_rows = x.rearrange("(p i) k -> p i k", i=ROW_TILES)
-
-        def load_x(i):
-            nc.sync.dma_start(out=x_sb[:, i : i + 2, :], in_=x_rows[:, i : i + 2, :])
-
-        load_x(0)
-        load_w1_scales(0)
+        nc.sync.dma_start(out=x_sb[:], in_=x_rows)
         load_w1(0)
-        load_x(2)
+        load_w1_scales(0)
         nc.scalar.activation(out=warm[:], in_=ones[:], func=ACT.Exp)
         load_gate_input(nc.scalar, 1, noise)
         load_gate_input(nc.scalar, 2, clean_logits)
@@ -117,11 +112,12 @@ def tile_mblfe_pa_e_kernel(
             load_w1(e)
         load_w2(0)
         load_w1(PLANES)
+        load_w1(PLANES + 1)
         load_w2_scales()
         for g in range(1, E // PLANES):
             load_w1_scales(g)
         for g in range(1, E // PLANES):
-            for e in range(g * PLANES + 1, min((g + 1) * PLANES + 1, E)):
+            for e in range(g * PLANES + 2, min((g + 1) * PLANES + 2, E)):
                 load_w1(e)
             load_w2(g)
         nc.sync.dma_start(
@@ -168,8 +164,8 @@ def tile_mblfe_pa_e_kernel(
 
         def sort_w1_scales(g):
             nc.vector.tensor_copy(
-                out=w1_planes[:, g, :].rearrange("p (t m) -> p t m", t=PACK),
-                in_=w1_raw_planes[:, g, :].rearrange("p (m t) -> p t m", t=PACK),
+                out=w1_planes[:, g, :].rearrange("p (t c i) -> p c t i", t=PACK, i=PACK),
+                in_=w1_raw_planes[:, g, :].rearrange("p (c i t) -> p c t i", t=PACK, i=PACK),
             )
 
 
@@ -231,26 +227,11 @@ def tile_mblfe_pa_e_kernel(
                 gate_steps.remove(step)
                 step()
 
-        group_x(0)
-        group_x(1)
-        quantise_x(0)
-        group_b1()
-        quantise_x(1)
-        sort_w1_scales(0)
-        sort_w1(0)
-        group_x(2)
-        group_x(3)
-        quantise_x(2)
-        logit_steps[0]()
-        quantise_x(3)
-        sort_w1(1)
-        logit_steps[1]()
-
         out_rows = out.rearrange("(p i) e l -> p i e l", i=ROW_TILES)
         half = ROW_TILES // 2
         pieces = [(0, 0, half), (0, half, half)]
-        pieces += [(e, 0, ROW_TILES) for e in range(1, E - 1)]
-        pieces += [(E - 1, 0, half), (E - 1, half, half)]
+        pieces += [(e, 0, ROW_TILES) for e in range(1, E - STORE)]
+        pieces += [(e, i0, half) for e in range(E - STORE, E) for i0 in (0, half)]
         sums, hidden, grouped, packed, products, biased = {}, {}, {}, {}, {}, {}
 
         def first_product(s, slots):
@@ -337,12 +318,17 @@ def tile_mblfe_pa_e_kernel(
         def store(tiles, experts):
             nc.sync.dma_start(out=out_rows[:, tiles, experts, :], in_=result[:, tiles, experts, :])
 
+        def on_vector(e, i):
+            if e == E - 1:
+                return i % 2 == 0
+            return e % VECTOR_EVERY == VECTOR_EVERY - 1 and e < E - STORE
+
         def weigh_and_store(s):
             e, i0, n = pieces[s]
             for i in range(n):
                 weighed = result[:, i0 + i, e, :]
                 gate = gates[:, i0 + i, e : e + 1]
-                if e % VECTOR_EVERY == VECTOR_EVERY - 1 and (e < E - 1 or i % 2 == 0):
+                if on_vector(e, i):
                     nc.vector.tensor_scalar_mul(out=weighed, in0=biased[s][:, i, :], scalar1=gate)
                 else:
                     nc.scalar.activation(out=weighed, in_=biased[s][:, i, :], func=ACT.Copy, scale=gate)
@@ -357,6 +343,21 @@ def tile_mblfe_pa_e_kernel(
                 sort_w1(e + 2)
             if i0 == 0 and e % PLANES == PLANES - 1 and e + 1 < E:
                 sort_w1_scales((e + 1) // PLANES)
+
+        group_x(0)
+        group_x(1)
+        quantise_x(0)
+        sort_w1(0)
+        quantise_x(1)
+        sort_w1_scales(0)
+        group_x(2)
+        group_x(3)
+        group_b1()
+        quantise_x(2)
+        logit_steps[0]()
+        quantise_x(3)
+        sort_w1(1)
+        logit_steps[1]()
 
         for s in range(len(pieces) + 4):
             if s < len(pieces):

from contextlib import ExitStack

import concourse.mybir as mybir
from concourse.masks import make_identity

F32 = mybir.dt.float32
BF16 = mybir.dt.bfloat16
I32 = mybir.dt.int32
U32 = mybir.dt.uint32
U8 = mybir.dt.uint8
FP8X4 = mybir.dt.float8_e4m3fn_x4
ALU = mybir.AluOpType
ACT = mybir.ActivationFunctionType
AX = mybir.AxisListType

P = 128
PACK = 4
B, D, E, H, L = 512, 512, 16, 512, 128
ROW_TILES = B // P
NOISE_EPS = 0.01
MEAN_EPS = 1e-8
PLANES = 4
STORE = 2
VECTOR_EVERY = 3
RUN = 8

FLOPS = 2 * E * B * D * H + 2 * E * B * H * L


def tile_mblfe_pa_e_kernel(
    tc, x, noise, clean_logits, noise_pre, W1_words, W1_scales, b1, W2_words, W2_scales, b2, out
):
    nc = tc.nc
    with ExitStack() as ctx:
        keep = ctx.enter_context(tc.tile_pool(name="keep", bufs=1))
        acts = ctx.enter_context(tc.tile_pool(name="acts", bufs=3))
        sorted_w1 = ctx.enter_context(tc.tile_pool(name="sorted_w1", bufs=4))
        z_banks = ctx.enter_context(tc.psum_pool(name="z_banks", bufs=6))
        y_banks = ctx.enter_context(tc.psum_pool(name="y_banks", bufs=2))
        ctx.enter_context(tc.manual_schedule())

        x_sb = keep.tile([P, ROW_TILES, D], BF16)
        x_grouped = keep.tile([P, ROW_TILES * P * PACK], BF16, align_bytes=64)
        x_codes = keep.tile([P, B], U32, align_bytes=64)
        x_plane = keep.tile([P, B], U8, align_bytes=64)
        w1_raw = keep.tile([P, E, H], U32, align_bytes=64)
        w1_raw_planes = keep.tile([P, E // PLANES, H], U8, align_bytes=64)
        w1_planes = keep.tile([P, E // PLANES, H], U8, align_bytes=64)
        w2_codes = keep.tile([P, E, L], U32, align_bytes=64)
        w2_planes = keep.tile([P, E, L], U8, align_bytes=64)
        b1_rows = keep.tile([P, H], BF16)
        b1_cols = keep.tile([P, E, PACK], BF16)
        b2_flat = keep.tile([P, PLANES * L], BF16)
        b2_rows = keep.tile([P, E * L], BF16)
        spread = keep.tile([P, P], BF16)
        gate_in = keep.tile([P, 3, ROW_TILES, E], BF16)
        result = keep.tile([P, ROW_TILES, E, L], F32)
        ident = keep.tile([P, P], F32)
        ones = keep.tile([P, 1], F32)
        warm = keep.tile([P, 1], F32)

        nc.vector.memset(b1_rows[:].bitcast(F32), 0.0)
        nc.vector.memset(ones[:], 1.0)
        nc.vector.memset(w1_raw_planes[:, 0, :].bitcast(I32), 0)
        nc.vector.memset(w1_raw_planes[:, 1:, :].rearrange("p g n -> p (g n)").bitcast(I32), 0)
        nc.vector.memset(w2_planes[:].bitcast(I32), 0)
        make_identity(nc, ident[:])

        def load_w1(e):
            nc.sync.dma_start(
                out=w1_raw[:, e, :].bitcast(I32),
                in_=W1_words[e].rearrange("p n t -> p (n t)").bitcast(I32),
            )

        def load_w1_scales(g):
            for q in range(4):
                nc.sync.dma_start(
                    out=w1_raw_planes[32 * q : 32 * q + 4 * PLANES, g, :].bitcast(I32),
                    in_=W1_scales[g * PLANES : (g + 1) * PLANES, 4 * q : 4 * q + 4, :].bitcast(I32),
                )

        def load_w2_scales():
            for q in range(4):
                nc.sync.dma_start(
                    out=w2_planes[32 * q : 32 * q + 4, :, :].bitcast(I32),
                    in_=W2_scales[:, 4 * q : 4 * q + 4, :].rearrange("g r n -> r g n").bitcast(I32),
                )

        def load_w2(g):
            es = slice(g * PLANES, (g + 1) * PLANES)
            nc.sync.dma_start(
                out=w2_codes[:, es, :].bitcast(I32),
                in_=W2_words[es].rearrange("g p n t -> p g (n t)").bitcast(I32),
            )

        def load_gate_input(queue, j, src):
            queue.dma_start(out=gate_in[:, j], in_=src.rearrange("(p i) e -> p i e", i=ROW_TILES))

        load_gate_input(nc.sync, 0, noise_pre)
        nc.gpsimd.dma_start(out=b1_rows[:E, :], in_=b1)
        x_rows = x.rearrange("(p i) k -> p i k", i=ROW_TILES)
        nc.sync.dma_start(out=x_sb[:], in_=x_rows)
        load_w1(0)
        load_w1_scales(0)
        nc.scalar.activation(out=warm[:], in_=ones[:], func=ACT.Exp)
        load_gate_input(nc.scalar, 1, noise)
        load_gate_input(nc.scalar, 2, clean_logits)
        nc.gpsimd.memset(b2_flat[:].bitcast(F32), 0.0)
        nc.gpsimd.memset(spread[:], 1.0)
        nc.gpsimd.dma_start(out=b2_flat[:1, :], in_=b2[:PLANES, :].rearrange("(o e) l -> o (e l)", o=1))
        for e in range(1, PLANES):
            load_w1(e)
        load_w2(0)
        load_w1(PLANES)
        load_w1(PLANES + 1)
        load_w2_scales()
        for g in range(1, E // PLANES):
            load_w1_scales(g)
        for g in range(1, E // PLANES):
            for e in range(g * PLANES + 2, min((g + 1) * PLANES + 2, E)):
                load_w1(e)
            load_w2(g)
        nc.sync.dma_start(
            out=b2_rows[:, PLANES * L :],
            in_=b2[PLANES:, :].rearrange("e l -> (e l)").partition_broadcast(P),
        )

        def flip(rows):
            flipped = z_banks.tile([P, 2, P], F32, tag="z")
            for u in range(2):
                nc.tensor.transpose(flipped[:, u, :], rows.bitcast(F32)[:, u : D // 2 : 2], ident[:])
            return flipped

        x_words = x_grouped[:].bitcast(F32).rearrange("q (i b u) -> q i b u", i=ROW_TILES, u=2)

        def group_x(i):
            xt = flip(x_sb[:, i, :])
            nc.vector.tensor_copy(out=x_words[:, i], in_=xt[:].rearrange("q u b -> q b u"))

        def quantise_x(i):
            rows = slice(i * P, (i + 1) * P)
            nc.vector.quantize_mx(
                out=x_codes[:, rows].bitcast(FP8X4),
                scales=x_plane[:, rows],
                in_=x_grouped[:, i * P * PACK : (i + 1) * P * PACK],
            )

        def group_b1():
            bt = flip(b1_rows[:])
            nc.vector.tensor_copy(
                out=b1_cols[:].rearrange("q e t -> q (e t)").bitcast(F32).rearrange("q (e u) -> q e u", u=2),
                in_=bt[:, :, :E].rearrange("q u e -> q e u"),
            )

        w1_codes = {}

        def sort_w1(e):
            codes = sorted_w1.tile([P, H], U32, align_bytes=64)
            nc.vector.tensor_copy(
                out=codes[:].bitcast(I32).rearrange("p (t c i) -> p c t i", t=PACK, i=PACK),
                in_=w1_raw[:, e, :].bitcast(I32).rearrange("p (c i t) -> p c t i", t=PACK, i=PACK),
            )
            w1_codes[e] = codes

        def sort_w1_scales(g):
            nc.vector.tensor_copy(
                out=w1_planes[:, g, :].rearrange("p (t c i) -> p c t i", t=PACK, i=PACK),
                in_=w1_raw_planes[:, g, :].rearrange("p (c i t) -> p c t i", t=PACK, i=PACK),
            )


        shape = [P, ROW_TILES, E]
        pre, noi, cln = gate_in[:, 0], gate_in[:, 1], gate_in[:, 2]
        mag = keep.tile(shape, F32)
        nc.scalar.activation(out=mag[:], in_=pre, func=ACT.Abs)
        decay = keep.tile(shape, F32)
        nc.scalar.activation(out=decay[:], in_=mag[:], func=ACT.Exp, scale=-1.0)
        log1p = keep.tile(shape, F32)
        nc.scalar.activation(out=log1p[:], in_=decay[:], func=ACT.Ln, bias=1.0)
        nc.scalar.activation(out=warm[:], in_=ones[:], func=ACT.Tanh)

        def over_experts(per_row):
            return per_row[:].unsqueeze(2).to_broadcast(shape)

        softplus = keep.tile(shape, F32)
        noisy = keep.tile(shape, F32)
        logits = keep.tile(shape, F32)
        top = keep.tile([P, ROW_TILES], F32)
        shifted = keep.tile(shape, F32)
        expd = keep.tile(shape, F32)
        esum = keep.tile([P, ROW_TILES], F32)
        cut = keep.tile([P, ROW_TILES], F32)
        alive = keep.tile(shape, F32)
        kept = keep.tile(shape, F32)
        ksum = keep.tile([P, ROW_TILES], F32)
        kinv = keep.tile([P, ROW_TILES], F32)
        gates = keep.tile(shape, F32)
        vec = nc.vector
        logit_steps = [
            lambda: vec.scalar_tensor_tensor(
                out=softplus[:], in0=pre, scalar=0.0, in1=log1p[:], op0=ALU.max, op1=ALU.add
            ),
            lambda: vec.scalar_tensor_tensor(
                out=noisy[:], in0=softplus[:], scalar=NOISE_EPS, in1=noi, op0=ALU.add, op1=ALU.mult
            ),
            lambda: vec.tensor_tensor(out=logits[:], in0=noisy[:], in1=cln, op=ALU.add),
            lambda: vec.tensor_reduce(out=top[:], in_=logits[:], axis=AX.X, op=ALU.max),
            lambda: vec.tensor_tensor(
                out=shifted[:], in0=logits[:], in1=over_experts(top), op=ALU.subtract
            ),
        ]
        gate_steps = logit_steps[2:] + [
            lambda: vec.tensor_reduce(out=esum[:], in_=expd[:], axis=AX.X, op=ALU.add),
            lambda: vec.tensor_scalar(
                out=cut[:], in0=esum[:], scalar1=1.0 / E - MEAN_EPS, scalar2=None, op0=ALU.mult
            ),
            lambda: vec.tensor_tensor(out=alive[:], in0=expd[:], in1=over_experts(cut), op=ALU.is_ge),
            lambda: vec.tensor_tensor(out=kept[:], in0=expd[:], in1=alive[:], op=ALU.mult),
            lambda: vec.tensor_reduce(out=ksum[:], in_=kept[:], axis=AX.X, op=ALU.add),
            lambda: vec.reciprocal(out=kinv[:], in_=ksum[:]),
            lambda: vec.tensor_tensor(out=gates[:], in0=kept[:], in1=over_experts(kinv), op=ALU.mult),
        ]

        def next_gate_step():
            if gate_steps:
                step = gate_steps[0]
                gate_steps.remove(step)
                step()

        out_rows = out.rearrange("(p i) e l -> p i e l", i=ROW_TILES)
        half = ROW_TILES // 2
        pieces = [(0, 0, half), (0, half, half)]
        pieces += [(e, 0, ROW_TILES) for e in range(1, E - STORE)]
        pieces += [(e, i0, half) for e in range(E - STORE, E) for i0 in (0, half)]
        sums, hidden, grouped, packed, products, biased = {}, {}, {}, {}, {}, {}

        def first_product(s, slots):
            e, i0, n = pieces[s]
            k = PACK * (e % PLANES)
            rows = slice(i0 * P, (i0 + n) * P)
            for t in slots:
                cols = slice(t * P, (t + 1) * P)
                z = z_banks.tile([P, n * P], F32, tag="z")
                nc.tensor.matmul_mx(
                    out=z[:],
                    lhsT=w1_codes[e][:, cols].bitcast(FP8X4),
                    lhsT_scale=w1_planes[k:, e // PLANES, cols],
                    rhs=x_codes[:, rows].bitcast(FP8X4),
                    rhs_scale=x_plane[:, rows],
                    start=True,
                    stop=True,
                )
                sums[(s, t)] = z

        def add_bias_and_tanh(s, slots):
            e, i0, n = pieces[s]
            if s not in hidden:
                ht = acts.tile([P, PACK, n * P], BF16)
                hidden[s] = ht
            for t in slots:
                nc.scalar.activation(
                    out=hidden[s][:, t, :], in_=sums[(s, t)][:], func=ACT.Tanh, bias=b1_cols[:, e, t : t + 1]
                )

        def group_hidden(s):
            e, i0, n = pieces[s]
            hg = acts.tile([P, n * P, PACK], BF16, align_bytes=64)
            nc.vector.tensor_copy(
                out=hg[:].rearrange("q (c i) t -> q c t i", i=RUN),
                in_=hidden[s][:].rearrange("q t (c i) -> q c t i", i=RUN),
            )
            grouped[s] = hg

        def quantise_hidden(s):
            e, i0, n = pieces[s]
            h_codes = acts.tile([P, n * P], U32, align_bytes=64)
            h_plane = acts.tile([P, n * P], U8, align_bytes=64)
            nc.vector.quantize_mx(
                out=h_codes[:].bitcast(FP8X4),
                scales=h_plane[:],
                in_=grouped[s][:].rearrange("q b t -> q (b t)"),
            )
            packed[s] = (h_codes, h_plane)

        def second_product(s):
            e, i0, n = pieces[s]
            h_codes, h_plane = packed[s]
            y = y_banks.tile([P, n, L], F32, tag="y")
            for i in range(n):
                rows = slice(i * P, (i + 1) * P)
                nc.tensor.matmul_mx(
                    out=y[:, i, :],
                    lhsT=h_codes[:, rows].bitcast(FP8X4),
                    lhsT_scale=h_plane[:, rows],
                    rhs=w2_codes[:, e, :].bitcast(FP8X4),
                    rhs_scale=w2_planes[:, e, :],
                    start=True,
                    stop=True,
                )
            products[s] = y

        def add_b2(s):
            e, i0, n = pieces[s]
            yb = acts.tile([P, n, L], F32)
            nc.vector.tensor_tensor(
                out=yb[:],
                in0=products[s][:],
                in1=b2_rows[:, e * L : (e + 1) * L].unsqueeze(1).to_broadcast([P, n, L]),
                op=ALU.add,
            )
            biased[s] = yb

        def spread_b2():
            bank = y_banks.tile([P, PLANES * L], BF16, tag="y")
            nc.tensor.matmul(bank[:], lhsT=spread[:], rhs=b2_flat[:], start=True, stop=True)
            nc.scalar.copy(b2_rows[:, : PLANES * L], bank[:])

        def store(tiles, experts):
            nc.sync.dma_start(out=out_rows[:, tiles, experts, :], in_=result[:, tiles, experts, :])

        def on_vector(e, i):
            if e == E - 1:
                return i % 2 == 0
            return e % VECTOR_EVERY == VECTOR_EVERY - 1 and e < E - STORE

        def weigh_and_store(s):
            e, i0, n = pieces[s]
            for i in range(n):
                weighed = result[:, i0 + i, e, :]
                gate = gates[:, i0 + i, e : e + 1]
                if on_vector(e, i):
                    nc.vector.tensor_scalar_mul(out=weighed, in0=biased[s][:, i, :], scalar1=gate)
                else:
                    nc.scalar.activation(out=weighed, in_=biased[s][:, i, :], func=ACT.Copy, scale=gate)
            if e >= E - STORE:
                store(slice(i0, i0 + n), slice(e, e + 1))
            elif e % STORE == STORE - 1:
                store(slice(0, ROW_TILES), slice(e + 1 - STORE, e + 1))

        def sort_next(s):
            e, i0, n = pieces[s]
            if i0 == 0 and e + 2 < E:
                sort_w1(e + 2)
            if i0 == 0 and e % PLANES == PLANES - 1 and e + 1 < E:
                sort_w1_scales((e + 1) // PLANES)

        group_x(0)
        group_x(1)
        quantise_x(0)
        sort_w1(0)
        quantise_x(1)
        sort_w1_scales(0)
        group_x(2)
        group_x(3)
        group_b1()
        quantise_x(2)
        logit_steps[0]()
        quantise_x(3)
        sort_w1(1)
        logit_steps[1]()

        for s in range(len(pieces) + 4):
            if s < len(pieces):
                first_product(s, (0, 1))
            if s == 3:
                nc.scalar.activation(out=expd[:], in_=shifted[:], func=ACT.Exp)
            if 0 <= s - 1 < len(pieces):
                add_bias_and_tanh(s - 1, (0, 1))
            if 0 <= s - 3 < len(pieces):
                second_product(s - 3)
            if s < len(pieces):
                first_product(s, (2, 3))
            if 0 <= s - 1 < len(pieces):
                add_bias_and_tanh(s - 1, (2, 3))
            if s == 1:
                spread_b2()
            if s < len(pieces):
                sort_next(s)
                next_gate_step()
            if 0 <= s - 2 < len(pieces):
                group_hidden(s - 2)
                if s >= 3:
                    next_gate_step()
            if 0 <= s - 3 < len(pieces):
                add_b2(s - 3)
                next_gate_step()
            if 0 <= s - 2 < len(pieces):
                quantise_hidden(s - 2)
                if s >= 3:
                    next_gate_step()
            if 0 <= s - 4 < len(pieces):
                weigh_and_store(s - 4)
